import numpy as np
import ml_dtypes


def mxq(x, axis, fmt="e4m3"):
    dtype, down = {"e4m3": (ml_dtypes.float8_e4m3fn, 7), "e5m2": (ml_dtypes.float8_e5m2, 14)}[fmt]
    v = np.moveaxis(np.asarray(x, np.float32).astype(ml_dtypes.bfloat16).astype(np.float64), axis, -1)
    blocks = v.reshape(v.shape[:-1] + (-1, 32))
    amax = np.abs(blocks).max(-1, keepdims=True)
    byte = np.maximum(np.where(amax > 0, np.frexp(amax)[1] - 1 + 127, 0) - down, 1)
    scale = np.exp2(byte - 127.0)
    codes = (blocks / scale).astype(np.float32).astype(dtype).astype(np.float64)
    return np.moveaxis((codes * scale).reshape(v.shape), -1, axis)


BF16 = ml_dtypes.bfloat16


def bf(x):
    return np.asarray(x, np.float32).astype(BF16)


def f64(x):
    return np.asarray(x).astype(np.float64)


B, C, H, W = 4, 128, 128, 128
M = H * W


def setup_inputs():
    noise = np.random.standard_normal((B, C, H, W))
    shared = np.random.standard_normal((B, 1, H, W))
    gain = np.random.standard_normal((B, C, 1, 1))
    offset = np.random.standard_normal((B, C, 1, 1))
    return {"x": bf(noise + 0.7 * gain * shared + 0.5 * offset)}


def reference(x):
    xf = f64(x).reshape(B, C, M)
    xc = xf - np.mean(xf, axis=2, keepdims=True)
    xq = mxq(xc, 2, "e4m3")
    return (xq @ xq.transpose(0, 2, 1)) / M

@@ -1,0 +1,217 @@
+from contextlib import ExitStack
+
+import concourse.mybir as mybir
+from concourse.masks import make_identity
+
+F32 = mybir.dt.float32
+BF16 = mybir.dt.bfloat16
+U32 = mybir.dt.uint32
+U8 = mybir.dt.uint8
+FP8X4 = mybir.dt.float8_e4m3fn_x4
+ALU = mybir.AluOpType
+ACT = mybir.ActivationFunctionType
+
+IMAGES = 4
+CHANNELS = 128
+POSITIONS = 16384
+FLOPS = 2 * IMAGES * CHANNELS * CHANNELS * POSITIONS
+
+P = 128
+UNITS = 2 * IMAGES
+UNIT_COLS = POSITIONS // 2
+PIECES_PER_UNIT = 4
+PIECES = UNITS * PIECES_PER_UNIT
+PIECE_COLS = UNIT_COLS // PIECES_PER_UNIT
+PIECE_WORDS = PIECE_COLS // 2
+BANK_WORDS = 512
+TRANSPOSES_PER_BANK = BANK_WORDS // P
+BANKS_PER_PIECE = PIECE_WORDS // BANK_WORDS
+PASSES_PER_PIECE = PIECE_WORDS // P
+VECTOR_SUM_COLS = 1344
+JOIN_LAG = 1
+CENTRE_LAG = PIECES_PER_UNIT + 1
+TRANSPOSE_LAG = CENTRE_LAG + 1
+GROUP_LAG = CENTRE_LAG + 2
+QUANTISE_LAG = CENTRE_LAG + 3
+MULTIPLY_LAG = CENTRE_LAG + 4
+
+
+def tile_covpool_k_kernel(tc, x, out):
+    nc = tc.nc
+    x_rows = x.rearrange("b c (j h) w -> (b c j) (h w)", j=2)
+
+    with ExitStack() as ctx:
+        consts = ctx.enter_context(tc.tile_pool(name="consts", bufs=1))
+        resident = ctx.enter_context(tc.tile_pool(name="resident", bufs=1))
+        grouped_pool = ctx.enter_context(tc.tile_pool(name="grouped", bufs=2 * PIECES_PER_UNIT))
+        mx_pool = ctx.enter_context(tc.tile_pool(name="mx", bufs=3))
+        y_pool = ctx.enter_context(tc.tile_pool(name="y", bufs=IMAGES))
+        work_psum = ctx.enter_context(tc.psum_pool(name="work_psum", bufs=6))
+        acc_psum = ctx.enter_context(tc.psum_pool(name="acc_psum", bufs=2))
+        ctx.enter_context(tc.manual_schedule())
+
+        x_sb = []
+        for u in range(UNITS):
+            x_unit = resident.tile([P, UNIT_COLS], BF16, name="x_unit%d" % u)
+            x_sb.append(x_unit)
+            for i in range(PIECES_PER_UNIT):
+                cols = slice(i * PIECE_COLS, (i + 1) * PIECE_COLS)
+                nc.sync.dma_start(out=x_unit[:, cols], in_=x_rows[u * P : (u + 1) * P, cols])
+
+        ident = consts.tile([P, P], F32)
+        make_identity(nc, ident[:])
+        ident_pairs = ident[:].rearrange("p (c j) -> p c j", j=2)
+        pair_cols = consts.tile([P, P // 2], F32)
+        nc.vector.tensor_tensor(
+            out=pair_cols[:], in0=ident_pairs[:, :, 0], in1=ident_pairs[:, :, 1], op=ALU.add
+        )
+        pair_mean = consts.tile([P, P // 2, 2], F32)
+        nc.vector.tensor_scalar(
+            out=pair_mean[:],
+            in0=pair_cols[:].unsqueeze(2).to_broadcast([P, P // 2, 2]),
+            scalar1=1.0 / POSITIONS,
+            scalar2=None,
+            op0=ALU.mult,
+        )
+
+        vector_sums = [
+            resident.tile([P, PIECES_PER_UNIT], F32, name="vector_sums%d" % u) for u in range(UNITS)
+        ]
+        scalar_sums = [
+            resident.tile([P, PIECES_PER_UNIT], F32, name="scalar_sums%d" % u) for u in range(UNITS)
+        ]
+        means = [resident.tile([P, 1], F32, name="mean%d" % u) for u in range(UNITS)]
+        banks = {}
+        grouped = {}
+        quantised = {}
+        acc = {}
+
+        def piece_of(x_unit, i):
+            return x_unit[:, i * PIECE_COLS : (i + 1) * PIECE_COLS]
+
+        def add_up(u, i):
+            piece = piece_of(x_sb[u], i)
+            nc.vector.tensor_scalar(
+                out=piece[:, :VECTOR_SUM_COLS],
+                in0=piece[:, :VECTOR_SUM_COLS],
+                scalar1=1.0,
+                scalar2=None,
+                op0=ALU.mult,
+                op1=ALU.add,
+                accum_out=vector_sums[u][:, i : i + 1],
+            )
+            nc.scalar.activation(
+                out=piece[:, VECTOR_SUM_COLS:],
+                in_=piece[:, VECTOR_SUM_COLS:],
+                func=ACT.Copy,
+                accum_out=scalar_sums[u][:, i : i + 1],
+            )
+
+        def join_halves(u):
+            mean_parts = work_psum.tile([P, PIECES_PER_UNIT], F32, tag="work")
+            pair_lhsT = pair_mean[:].rearrange("p c j -> p (c j)")
+            nc.tensor.matmul(
+                out=mean_parts[:], lhsT=pair_lhsT, rhs=vector_sums[u][:], start=True, stop=False
+            )
+            nc.tensor.matmul(
+                out=mean_parts[:], lhsT=pair_lhsT, rhs=scalar_sums[u][:], start=False, stop=True
+            )
+            return mean_parts
+
+        def finish_mean(u, mean_parts):
+            nc.vector.tensor_reduce(
+                out=means[u][:], in_=mean_parts[:], axis=mybir.AxisListType.X, op=ALU.add
+            )
+
+        def centre(u, i):
+            piece = piece_of(x_sb[u], i)
+            nc.vector.tensor_scalar(
+                out=piece, in0=piece, scalar1=means[u][:, 0:1], scalar2=None, op0=ALU.subtract
+            )
+
+        def transpose(u, i):
+            words = x_sb[u][:].bitcast(F32)
+            banks[(u, i)] = []
+            for n in range(BANKS_PER_PIECE):
+                bank = work_psum.tile([P, TRANSPOSES_PER_BANK, P], F32, tag="work")
+                for t in range(TRANSPOSES_PER_BANK):
+                    first = i * PIECE_WORDS + (n * TRANSPOSES_PER_BANK + t) * P
+                    nc.tensor.transpose(bank[:, t, :], words[:, first : first + P], ident[:])
+                banks[(u, i)].append(bank)
+
+        def group(u, i):
+            b, r = divmod(u, 2)
+            if r == 0:
+                grouped_tile = grouped_pool.tile(
+                    [P, 2 * PIECE_WORDS], F32, tag="grouped", align_bytes=64
+                )
+                grouped[(b, i)] = grouped_tile
+            by_pass = grouped[(b, i)][:].rearrange(
+                "p (g r w) -> p g r w", g=PASSES_PER_PIECE, r=2
+            )
+            for n in range(BANKS_PER_PIECE):
+                passes = slice(n * TRANSPOSES_PER_BANK, (n + 1) * TRANSPOSES_PER_BANK)
+                nc.scalar.copy(out=by_pass[:, passes, r, :], in_=banks[(u, i)][n][:])
+
+        def quantise(b, i):
+            codes = mx_pool.tile([P, PASSES_PER_PIECE * CHANNELS], U32, tag="codes", align_bytes=64)
+            scales = mx_pool.tile([P, PASSES_PER_PIECE * CHANNELS], U8, tag="scales", align_bytes=64)
+            nc.vector.quantize_mx(
+                out=codes[:].bitcast(FP8X4), scales=scales[:], in_=grouped[(b, i)][:].bitcast(BF16)
+            )
+            quantised[(b, i)] = (codes, scales)
+
+        def multiply(b, i):
+            if i == 0:
+                acc_tile = acc_psum.tile([CHANNELS, CHANNELS], F32, tag="acc")
+                acc[b] = acc_tile
+            codes, scales = quantised[(b, i)]
+            for g in range(PASSES_PER_PIECE):
+                cols = slice(g * CHANNELS, (g + 1) * CHANNELS)
+                nc.tensor.matmul_mx(
+                    out=acc[b][:],
+                    lhsT=codes[:, cols].bitcast(FP8X4),
+                    lhsT_scale=scales[:, cols],
+                    rhs=codes[:, cols].bitcast(FP8X4),
+                    rhs_scale=scales[:, cols],
+                    start=(i == 0 and g == 0),
+                    stop=(i == PIECES_PER_UNIT - 1 and g == PASSES_PER_PIECE - 1),
+                )
+
+        def store(b):
+            y_sb = y_pool.tile([CHANNELS, CHANNELS], F32, tag="y")
+            nc.scalar.activation(out=y_sb[:], in_=acc[b][:], func=ACT.Copy, scale=1.0 / POSITIONS)
+            nc.sync.dma_start(out=out[b], in_=y_sb[:])
+
+        def piece_at(s, lag):
+            if 0 <= s - lag < PIECES:
+                return divmod(s - lag, PIECES_PER_UNIT)
+            return None
+
+        mean_parts_of = {}
+        for s in range(PIECES + MULTIPLY_LAG):
+            to_quantise = piece_at(s, QUANTISE_LAG)
+            if to_quantise is not None and to_quantise[0] % 2 == 1:
+                quantise(to_quantise[0] // 2, to_quantise[1])
+            to_add_up = piece_at(s, 0)
+            if to_add_up is not None:
+                add_up(to_add_up[0], to_add_up[1])
+            to_join = piece_at(s, JOIN_LAG)
+            if to_join is not None and to_join[1] == PIECES_PER_UNIT - 1:
+                mean_parts_of[to_join[0]] = join_halves(to_join[0])
+            to_centre = piece_at(s, CENTRE_LAG)
+            if to_centre is not None:
+                if to_centre[1] == 0:
+                    finish_mean(to_centre[0], mean_parts_of[to_centre[0]])
+                centre(to_centre[0], to_centre[1])
+            to_transpose = piece_at(s, TRANSPOSE_LAG)
+            if to_transpose is not None:
+                transpose(to_transpose[0], to_transpose[1])
+            to_group = piece_at(s, GROUP_LAG)
+            if to_group is not None:
+                group(to_group[0], to_group[1])
+            to_multiply = piece_at(s, MULTIPLY_LAG)
+            if to_multiply is not None and to_multiply[0] % 2 == 1:
+                multiply(to_multiply[0] // 2, to_multiply[1])
+                if to_multiply[1] == PIECES_PER_UNIT - 1:
+                    store(to_multiply[0] // 2)

@@ -45,6 +45,7 @@ def tile_covpool_k_kernel(tc, x, out):
         resident = ctx.enter_context(tc.tile_pool(name="resident", bufs=1))
         grouped_pool = ctx.enter_context(tc.tile_pool(name="grouped", bufs=2 * PIECES_PER_UNIT))
         mx_pool = ctx.enter_context(tc.tile_pool(name="mx", bufs=3))
+        scratch = ctx.enter_context(tc.tile_pool(name="scratch", bufs=2))
         y_pool = ctx.enter_context(tc.tile_pool(name="y", bufs=IMAGES))
         work_psum = ctx.enter_context(tc.psum_pool(name="work_psum", bufs=6))
         acc_psum = ctx.enter_context(tc.psum_pool(name="acc_psum", bufs=2))
@@ -91,11 +92,12 @@ def tile_covpool_k_kernel(tc, x, out):
 
         def add_up(u, i):
             piece = piece_of(x_sb[u], i)
-            nc.vector.tensor_scalar(
-                out=piece[:, :VECTOR_SUM_COLS],
-                in0=piece[:, :VECTOR_SUM_COLS],
-                scalar1=1.0,
-                scalar2=None,
+            pair_sums = scratch.tile([P, VECTOR_SUM_COLS // 2], F32, tag="pair_sums")
+            nc.vector.scalar_tensor_tensor(
+                out=pair_sums[:],
+                in0=piece[:, : VECTOR_SUM_COLS // 2],
+                scalar=1.0,
+                in1=piece[:, VECTOR_SUM_COLS // 2 : VECTOR_SUM_COLS],
                 op0=ALU.mult,
                 op1=ALU.add,
                 accum_out=vector_sums[u][:, i : i + 1],

@@ -32,8 +32,12 @@ JOIN_LAG = 1
 CENTRE_LAG = PIECES_PER_UNIT + 1
 TRANSPOSE_LAG = CENTRE_LAG + 1
 GROUP_LAG = CENTRE_LAG + 2
-QUANTISE_LAG = CENTRE_LAG + 3
-MULTIPLY_LAG = CENTRE_LAG + 4
+CALLS = IMAGES * PIECES_PER_UNIT
+STEPS_PER_CALL = PIECES // CALLS
+FIRST_CALL_STEP = PIECES_PER_UNIT + GROUP_LAG + 2
+MULTIPLY_LAG = 1
+STORE_LAG = 2
+LAST_STEP = FIRST_CALL_STEP + (CALLS - 1) * STEPS_PER_CALL + STORE_LAG
 
 
 def tile_covpool_k_kernel(tc, x, out):
@@ -45,7 +49,6 @@ def tile_covpool_k_kernel(tc, x, out):
         resident = ctx.enter_context(tc.tile_pool(name="resident", bufs=1))
         grouped_pool = ctx.enter_context(tc.tile_pool(name="grouped", bufs=2 * PIECES_PER_UNIT))
         mx_pool = ctx.enter_context(tc.tile_pool(name="mx", bufs=3))
-        scratch = ctx.enter_context(tc.tile_pool(name="scratch", bufs=2))
         y_pool = ctx.enter_context(tc.tile_pool(name="y", bufs=IMAGES))
         work_psum = ctx.enter_context(tc.psum_pool(name="work_psum", bufs=6))
         acc_psum = ctx.enter_context(tc.psum_pool(name="acc_psum", bufs=2))
@@ -92,12 +95,11 @@ def tile_covpool_k_kernel(tc, x, out):
 
         def add_up(u, i):
             piece = piece_of(x_sb[u], i)
-            pair_sums = scratch.tile([P, VECTOR_SUM_COLS // 2], F32, tag="pair_sums")
-            nc.vector.scalar_tensor_tensor(
-                out=pair_sums[:],
-                in0=piece[:, : VECTOR_SUM_COLS // 2],
-                scalar=1.0,
-                in1=piece[:, VECTOR_SUM_COLS // 2 : VECTOR_SUM_COLS],
+            nc.vector.tensor_scalar(
+                out=piece[:, :VECTOR_SUM_COLS],
+                in0=piece[:, :VECTOR_SUM_COLS],
+                scalar1=1.0,
+                scalar2=None,
                 op0=ALU.mult,
                 op1=ALU.add,
                 accum_out=vector_sums[u][:, i : i + 1],
@@ -190,14 +192,17 @@ def tile_covpool_k_kernel(tc, x, out):
                 return divmod(s - lag, PIECES_PER_UNIT)
             return None
 
+        def call_at(s, lag):
+            steps = s - lag - FIRST_CALL_STEP
+            if steps >= 0 and steps % STEPS_PER_CALL == 0 and steps // STEPS_PER_CALL < CALLS:
+                return divmod(steps // STEPS_PER_CALL, PIECES_PER_UNIT)
+            return None
+
         mean_parts_of = {}
-        for s in range(PIECES + MULTIPLY_LAG):
-            to_quantise = piece_at(s, QUANTISE_LAG)
-            if to_quantise is not None and to_quantise[0] % 2 == 1:
-                quantise(to_quantise[0] // 2, to_quantise[1])
-            to_add_up = piece_at(s, 0)
-            if to_add_up is not None:
-                add_up(to_add_up[0], to_add_up[1])
+        for s in range(LAST_STEP + 1):
+            to_quantise = call_at(s, 0)
+            if to_quantise is not None:
+                quantise(to_quantise[0], to_quantise[1])
             to_join = piece_at(s, JOIN_LAG)
             if to_join is not None and to_join[1] == PIECES_PER_UNIT - 1:
                 mean_parts_of[to_join[0]] = join_halves(to_join[0])
@@ -212,8 +217,12 @@ def tile_covpool_k_kernel(tc, x, out):
             to_group = piece_at(s, GROUP_LAG)
             if to_group is not None:
                 group(to_group[0], to_group[1])
-            to_multiply = piece_at(s, MULTIPLY_LAG)
-            if to_multiply is not None and to_multiply[0] % 2 == 1:
-                multiply(to_multiply[0] // 2, to_multiply[1])
-                if to_multiply[1] == PIECES_PER_UNIT - 1:
-                    store(to_multiply[0] // 2)
+            to_multiply = call_at(s, MULTIPLY_LAG)
+            if to_multiply is not None:
+                multiply(to_multiply[0], to_multiply[1])
+            to_store = call_at(s, STORE_LAG)
+            if to_store is not None and to_store[1] == PIECES_PER_UNIT - 1:
+                store(to_store[0])
+            to_add_up = piece_at(s, 0)
+            if to_add_up is not None:
+                add_up(to_add_up[0], to_add_up[1])

@@ -17,24 +17,32 @@ POSITIONS = 16384
 FLOPS = 2 * IMAGES * CHANNELS * CHANNELS * POSITIONS
 
 P = 128
-UNITS = 2 * IMAGES
-UNIT_COLS = POSITIONS // 2
-PIECES_PER_UNIT = 4
+QUARTERS = 4
+UNIT_CHANNELS = P // QUARTERS
+UNITS_PER_IMAGE = CHANNELS // UNIT_CHANNELS
+UNITS = IMAGES * UNITS_PER_IMAGE
+UNIT_COLS = POSITIONS // QUARTERS
+PIECES_PER_UNIT = 2
 PIECES = UNITS * PIECES_PER_UNIT
 PIECE_COLS = UNIT_COLS // PIECES_PER_UNIT
 PIECE_WORDS = PIECE_COLS // 2
 BANK_WORDS = 512
 TRANSPOSES_PER_BANK = BANK_WORDS // P
 BANKS_PER_PIECE = PIECE_WORDS // BANK_WORDS
-PASSES_PER_PIECE = PIECE_WORDS // P
-VECTOR_SUM_COLS = 1344
-JOIN_LAG = 1
-CENTRE_LAG = PIECES_PER_UNIT + 1
-TRANSPOSE_LAG = CENTRE_LAG + 1
-GROUP_LAG = CENTRE_LAG + 2
-CALLS = IMAGES * PIECES_PER_UNIT
+BANKS_PER_UNIT = BANKS_PER_PIECE * PIECES_PER_UNIT
+MX_WORDS_PER_ROW = QUARTERS // 2
+PASSES_PER_BANK = TRANSPOSES_PER_BANK * MX_WORDS_PER_ROW
+UNIT_PASS_WORDS = 2 * UNIT_CHANNELS
+TENSOR_SUM_COLS = 1536
+SCALAR_SUM_COLS = 768
+SPREAD_LAG = 1
+JOIN_LAG = 2
+CENTRE_LAG = 4
+TRANSPOSE_LAG = 5
+GROUP_LAG = 6
+CALLS = IMAGES * BANKS_PER_UNIT
 STEPS_PER_CALL = PIECES // CALLS
-FIRST_CALL_STEP = PIECES_PER_UNIT + GROUP_LAG + 2
+FIRST_CALL_STEP = (UNITS_PER_IMAGE - 1) * PIECES_PER_UNIT + GROUP_LAG + 1
 MULTIPLY_LAG = 1
 STORE_LAG = 2
 LAST_STEP = FIRST_CALL_STEP + (CALLS - 1) * STEPS_PER_CALL + STORE_LAG
@@ -42,15 +50,17 @@ LAST_STEP = FIRST_CALL_STEP + (CALLS - 1) * STEPS_PER_CALL + STORE_LAG
 
 def tile_covpool_k_kernel(tc, x, out):
     nc = tc.nc
-    x_rows = x.rearrange("b c (j h) w -> (b c j) (h w)", j=2)
+    x_rows = x.rearrange("b c (j h) w -> (b c j) (h w)", j=QUARTERS)
 
     with ExitStack() as ctx:
         consts = ctx.enter_context(tc.tile_pool(name="consts", bufs=1))
         resident = ctx.enter_context(tc.tile_pool(name="resident", bufs=1))
-        grouped_pool = ctx.enter_context(tc.tile_pool(name="grouped", bufs=2 * PIECES_PER_UNIT))
+        spread_pool = ctx.enter_context(tc.tile_pool(name="spread", bufs=2))
+        grouped_pool = ctx.enter_context(tc.tile_pool(name="grouped", bufs=2 * BANKS_PER_UNIT))
         mx_pool = ctx.enter_context(tc.tile_pool(name="mx", bufs=3))
         y_pool = ctx.enter_context(tc.tile_pool(name="y", bufs=IMAGES))
-        work_psum = ctx.enter_context(tc.psum_pool(name="work_psum", bufs=6))
+        bank_psum = ctx.enter_context(tc.psum_pool(name="bank_psum", bufs=2 * BANKS_PER_PIECE))
+        stat_psum = ctx.enter_context(tc.psum_pool(name="stat_psum", bufs=1))
         acc_psum = ctx.enter_context(tc.psum_pool(name="acc_psum", bufs=2))
         ctx.enter_context(tc.manual_schedule())
 
@@ -64,113 +74,155 @@ def tile_covpool_k_kernel(tc, x, out):
 
         ident = consts.tile([P, P], F32)
         make_identity(nc, ident[:])
-        ident_pairs = ident[:].rearrange("p (c j) -> p c j", j=2)
-        pair_cols = consts.tile([P, P // 2], F32)
-        nc.vector.tensor_tensor(
-            out=pair_cols[:], in0=ident_pairs[:, :, 0], in1=ident_pairs[:, :, 1], op=ALU.add
+        by_mx_word = consts.tile([P, P], F32)
+        nc.vector.tensor_copy(
+            out=by_mx_word[:].rearrange("p (v c j) -> p v c j", v=MX_WORDS_PER_ROW, j=2),
+            in_=ident[:].rearrange("p (c v j) -> p v c j", v=MX_WORDS_PER_ROW, j=2),
         )
-        pair_mean = consts.tile([P, P // 2, 2], F32)
+        same_channel = consts.tile([P, UNIT_CHANNELS], F32)
+        nc.vector.tensor_reduce(
+            out=same_channel[:],
+            in_=ident[:].rearrange("p (c j) -> p c j", j=QUARTERS),
+            axis=mybir.AxisListType.X,
+            op=ALU.add,
+        )
+        same_channel_bf = consts.tile([P, UNIT_CHANNELS], BF16)
+        nc.vector.tensor_copy(out=same_channel_bf[:], in_=same_channel[:])
+        quarter_mean = consts.tile([P, UNIT_CHANNELS, QUARTERS], F32)
         nc.vector.tensor_scalar(
-            out=pair_mean[:],
-            in0=pair_cols[:].unsqueeze(2).to_broadcast([P, P // 2, 2]),
+            out=quarter_mean[:],
+            in0=same_channel[:].unsqueeze(2).to_broadcast([P, UNIT_CHANNELS, QUARTERS]),
             scalar1=1.0 / POSITIONS,
             scalar2=None,
             op0=ALU.mult,
         )
+        one_over_positions = consts.tile([P, 1], F32)
+        nc.vector.memset(one_over_positions[:], 1.0 / POSITIONS)
 
-        vector_sums = [
-            resident.tile([P, PIECES_PER_UNIT], F32, name="vector_sums%d" % u) for u in range(UNITS)
-        ]
-        scalar_sums = [
-            resident.tile([P, PIECES_PER_UNIT], F32, name="scalar_sums%d" % u) for u in range(UNITS)
-        ]
-        means = [resident.tile([P, 1], F32, name="mean%d" % u) for u in range(UNITS)]
+        vector_sums = resident.tile([P, UNITS], F32)
+        scalar_sums = resident.tile([P, UNITS], F32)
+        means = resident.tile([P, UNITS], F32)
+        column_sums = {}
+        spread_sums = {}
+        mean_psum = {}
         banks = {}
         grouped = {}
         quantised = {}
         acc = {}
 
-        def piece_of(x_unit, i):
-            return x_unit[:, i * PIECE_COLS : (i + 1) * PIECE_COLS]
+        def tensor_add_up(u):
+            sums = stat_psum.tile([P, UNIT_CHANNELS], F32, tag="column_sums")
+            column_sums[u] = sums
+            blocks = TENSOR_SUM_COLS // P
+            for k in range(blocks):
+                nc.tensor.matmul(
+                    out=sums[:],
+                    lhsT=x_sb[u][:, k * P : (k + 1) * P],
+                    rhs=same_channel_bf[:],
+                    start=(k == 0),
+                    stop=(k == blocks - 1),
+                )
 
-        def add_up(u, i):
-            piece = piece_of(x_sb[u], i)
+        def add_up(u):
+            scalar_cols = x_sb[u][:, TENSOR_SUM_COLS : TENSOR_SUM_COLS + SCALAR_SUM_COLS]
+            vector_cols = x_sb[u][:, TENSOR_SUM_COLS + SCALAR_SUM_COLS :]
             nc.vector.tensor_scalar(
-                out=piece[:, :VECTOR_SUM_COLS],
-                in0=piece[:, :VECTOR_SUM_COLS],
+                out=vector_cols,
+                in0=vector_cols,
                 scalar1=1.0,
                 scalar2=None,
                 op0=ALU.mult,
                 op1=ALU.add,
-                accum_out=vector_sums[u][:, i : i + 1],
+                accum_out=vector_sums[:, u : u + 1],
             )
             nc.scalar.activation(
-                out=piece[:, VECTOR_SUM_COLS:],
-                in_=piece[:, VECTOR_SUM_COLS:],
-                func=ACT.Copy,
-                accum_out=scalar_sums[u][:, i : i + 1],
+                out=scalar_cols, in_=scalar_cols, func=ACT.Copy, accum_out=scalar_sums[:, u : u + 1]
             )
 
-        def join_halves(u):
-            mean_parts = work_psum.tile([P, PIECES_PER_UNIT], F32, tag="work")
-            pair_lhsT = pair_mean[:].rearrange("p c j -> p (c j)")
-            nc.tensor.matmul(
-                out=mean_parts[:], lhsT=pair_lhsT, rhs=vector_sums[u][:], start=True, stop=False
+        def spread(u):
+            repeated = spread_pool.tile([P, UNIT_CHANNELS, QUARTERS], F32, tag="spread")
+            spread_sums[u] = repeated
+            nc.scalar.copy(
+                out=repeated[:],
+                in_=column_sums[u][:].unsqueeze(2).to_broadcast([P, UNIT_CHANNELS, QUARTERS]),
             )
-            nc.tensor.matmul(
-                out=mean_parts[:], lhsT=pair_lhsT, rhs=scalar_sums[u][:], start=False, stop=True
-            )
-            return mean_parts
 
-        def finish_mean(u, mean_parts):
-            nc.vector.tensor_reduce(
-                out=means[u][:], in_=mean_parts[:], axis=mybir.AxisListType.X, op=ALU.add
+        def join(u):
+            mean_of_unit = stat_psum.tile([P, 1], F32, tag="mean")
+            mean_psum[u] = mean_of_unit
+            quarters_lhsT = quarter_mean[:].rearrange("p c j -> p (c j)")
+            nc.tensor.matmul(
+                out=mean_of_unit[:],
+                lhsT=quarters_lhsT,
+                rhs=vector_sums[:, u : u + 1],
+                start=True,
+                stop=False,
+            )
+            nc.tensor.matmul(
+                out=mean_of_unit[:],
+                lhsT=quarters_lhsT,
+                rhs=scalar_sums[:, u : u + 1],
+                start=False,
+                stop=False,
+            )
+            nc.tensor.matmul(
+                out=mean_of_unit[:],
+                lhsT=spread_sums[u][:].rearrange("p c j -> p (c j)"),
+                rhs=one_over_positions[:],
+                start=False,
+                stop=True,
             )
 
         def centre(u, i):
-            piece = piece_of(x_sb[u], i)
+            if i == 0:
+                nc.vector.tensor_copy(out=means[:, u : u + 1], in_=mean_psum[u][:])
+            piece = x_sb[u][:, i * PIECE_COLS : (i + 1) * PIECE_COLS]
             nc.vector.tensor_scalar(
-                out=piece, in0=piece, scalar1=means[u][:, 0:1], scalar2=None, op0=ALU.subtract
+                out=piece, in0=piece, scalar1=means[:, u : u + 1], scalar2=None, op0=ALU.subtract
             )
 
         def transpose(u, i):
             words = x_sb[u][:].bitcast(F32)
             banks[(u, i)] = []
             for n in range(BANKS_PER_PIECE):
-                bank = work_psum.tile([P, TRANSPOSES_PER_BANK, P], F32, tag="work")
+                bank = bank_psum.tile([P, TRANSPOSES_PER_BANK, P], F32, tag="bank")
                 for t in range(TRANSPOSES_PER_BANK):
                     first = i * PIECE_WORDS + (n * TRANSPOSES_PER_BANK + t) * P
-                    nc.tensor.transpose(bank[:, t, :], words[:, first : first + P], ident[:])
+                    nc.tensor.transpose(bank[:, t, :], words[:, first : first + P], by_mx_word[:])
                 banks[(u, i)].append(bank)
 
         def group(u, i):
-            b, r = divmod(u, 2)
-            if r == 0:
-                grouped_tile = grouped_pool.tile(
-                    [P, 2 * PIECE_WORDS], F32, tag="grouped", align_bytes=64
-                )
-                grouped[(b, i)] = grouped_tile
-            by_pass = grouped[(b, i)][:].rearrange(
-                "p (g r w) -> p g r w", g=PASSES_PER_PIECE, r=2
-            )
+            b, part = divmod(u, UNITS_PER_IMAGE)
             for n in range(BANKS_PER_PIECE):
-                passes = slice(n * TRANSPOSES_PER_BANK, (n + 1) * TRANSPOSES_PER_BANK)
-                nc.scalar.copy(out=by_pass[:, passes, r, :], in_=banks[(u, i)][n][:])
+                call = (b, i * BANKS_PER_PIECE + n)
+                if part == 0:
+                    grouped_tile = grouped_pool.tile(
+                        [P, PASSES_PER_BANK * 2 * CHANNELS], F32, tag="grouped", align_bytes=64
+                    )
+                    grouped[call] = grouped_tile
+                by_pass = grouped[call][:].rearrange(
+                    "p (g u w) -> p g u w", g=PASSES_PER_BANK, u=UNITS_PER_IMAGE
+                )
+                nc.scalar.copy(
+                    out=by_pass[:, :, part, :],
+                    in_=banks[(u, i)][n][:].rearrange("p t (v w) -> p (t v) w", v=MX_WORDS_PER_ROW),
+                )
 
-        def quantise(b, i):
-            codes = mx_pool.tile([P, PASSES_PER_PIECE * CHANNELS], U32, tag="codes", align_bytes=64)
-            scales = mx_pool.tile([P, PASSES_PER_PIECE * CHANNELS], U8, tag="scales", align_bytes=64)
+        def quantise(call):
+            codes = mx_pool.tile([P, PASSES_PER_BANK * CHANNELS], U32, tag="codes", align_bytes=64)
+            scales = mx_pool.tile([P, PASSES_PER_BANK * CHANNELS], U8, tag="scales", align_bytes=64)
             nc.vector.quantize_mx(
-                out=codes[:].bitcast(FP8X4), scales=scales[:], in_=grouped[(b, i)][:].bitcast(BF16)
+                out=codes[:].bitcast(FP8X4), scales=scales[:], in_=grouped[call][:].bitcast(BF16)
             )
-            quantised[(b, i)] = (codes, scales)
+            quantised[call] = (codes, scales)
 
-        def multiply(b, i):
-            if i == 0:
+        def multiply(call):
+            b, n = call
+            if n == 0:
                 acc_tile = acc_psum.tile([CHANNELS, CHANNELS], F32, tag="acc")
                 acc[b] = acc_tile
-            codes, scales = quantised[(b, i)]
-            for g in range(PASSES_PER_PIECE):
+            codes, scales = quantised[call]
+            for g in range(PASSES_PER_BANK):
                 cols = slice(g * CHANNELS, (g + 1) * CHANNELS)
                 nc.tensor.matmul_mx(
                     out=acc[b][:],
@@ -178,8 +230,8 @@ def tile_covpool_k_kernel(tc, x, out):
                     lhsT_scale=scales[:, cols],
                     rhs=codes[:, cols].bitcast(FP8X4),
                     rhs_scale=scales[:, cols],
-                    start=(i == 0 and g == 0),
-                    stop=(i == PIECES_PER_UNIT - 1 and g == PASSES_PER_PIECE - 1),
+                    start=(n == 0 and g == 0),
+                    stop=(n == BANKS_PER_UNIT - 1 and g == PASSES_PER_BANK - 1),
                 )
 
         def store(b):
@@ -195,21 +247,23 @@ def tile_covpool_k_kernel(tc, x, out):
         def call_at(s, lag):
             steps = s - lag - FIRST_CALL_STEP
             if steps >= 0 and steps % STEPS_PER_CALL == 0 and steps // STEPS_PER_CALL < CALLS:
-                return divmod(steps // STEPS_PER_CALL, PIECES_PER_UNIT)
+                return divmod(steps // STEPS_PER_CALL, BANKS_PER_UNIT)
             return None
 
-        mean_parts_of = {}
+        first_piece = 0
+        last_piece = PIECES_PER_UNIT - 1
         for s in range(LAST_STEP + 1):
             to_quantise = call_at(s, 0)
             if to_quantise is not None:
-                quantise(to_quantise[0], to_quantise[1])
+                quantise(to_quantise)
+            to_spread = piece_at(s, SPREAD_LAG)
+            if to_spread is not None and to_spread[1] == first_piece:
+                spread(to_spread[0])
             to_join = piece_at(s, JOIN_LAG)
-            if to_join is not None and to_join[1] == PIECES_PER_UNIT - 1:
-                mean_parts_of[to_join[0]] = join_halves(to_join[0])
+            if to_join is not None and to_join[1] == last_piece:
+                join(to_join[0])
             to_centre = piece_at(s, CENTRE_LAG)
             if to_centre is not None:
-                if to_centre[1] == 0:
-                    finish_mean(to_centre[0], mean_parts_of[to_centre[0]])
                 centre(to_centre[0], to_centre[1])
             to_transpose = piece_at(s, TRANSPOSE_LAG)
             if to_transpose is not None:
@@ -219,10 +273,12 @@ def tile_covpool_k_kernel(tc, x, out):
                 group(to_group[0], to_group[1])
             to_multiply = call_at(s, MULTIPLY_LAG)
             if to_multiply is not None:
-                multiply(to_multiply[0], to_multiply[1])
+                multiply(to_multiply)
             to_store = call_at(s, STORE_LAG)
-            if to_store is not None and to_store[1] == PIECES_PER_UNIT - 1:
+            if to_store is not None and to_store[1] == BANKS_PER_UNIT - 1:
                 store(to_store[0])
-            to_add_up = piece_at(s, 0)
-            if to_add_up is not None:
-                add_up(to_add_up[0], to_add_up[1])
+            loaded = piece_at(s, 0)
+            if loaded is not None and loaded[1] == first_piece:
+                tensor_add_up(loaded[0])
+            if loaded is not None and loaded[1] == last_piece:
+                add_up(loaded[0])

@@ -17,32 +17,26 @@ POSITIONS = 16384
 FLOPS = 2 * IMAGES * CHANNELS * CHANNELS * POSITIONS
 
 P = 128
-QUARTERS = 4
-UNIT_CHANNELS = P // QUARTERS
-UNITS_PER_IMAGE = CHANNELS // UNIT_CHANNELS
-UNITS = IMAGES * UNITS_PER_IMAGE
-UNIT_COLS = POSITIONS // QUARTERS
-PIECES_PER_UNIT = 2
+UNITS = 2 * IMAGES
+UNIT_COLS = POSITIONS // 2
+PIECES_PER_UNIT = 4
 PIECES = UNITS * PIECES_PER_UNIT
 PIECE_COLS = UNIT_COLS // PIECES_PER_UNIT
 PIECE_WORDS = PIECE_COLS // 2
 BANK_WORDS = 512
 TRANSPOSES_PER_BANK = BANK_WORDS // P
 BANKS_PER_PIECE = PIECE_WORDS // BANK_WORDS
-BANKS_PER_UNIT = BANKS_PER_PIECE * PIECES_PER_UNIT
-MX_WORDS_PER_ROW = QUARTERS // 2
-PASSES_PER_BANK = TRANSPOSES_PER_BANK * MX_WORDS_PER_ROW
-UNIT_PASS_WORDS = 2 * UNIT_CHANNELS
-TENSOR_SUM_COLS = 1536
-SCALAR_SUM_COLS = 768
+PASSES_PER_PIECE = PIECE_WORDS // P
+TENSOR_SUM_COLS = 384
+VECTOR_SUM_COLS = 1152
 SPREAD_LAG = 1
 JOIN_LAG = 2
-CENTRE_LAG = 4
-TRANSPOSE_LAG = 5
-GROUP_LAG = 6
-CALLS = IMAGES * BANKS_PER_UNIT
+CENTRE_LAG = PIECES_PER_UNIT + 2
+TRANSPOSE_LAG = CENTRE_LAG + 1
+GROUP_LAG = CENTRE_LAG + 2
+CALLS = IMAGES * PIECES_PER_UNIT
 STEPS_PER_CALL = PIECES // CALLS
-FIRST_CALL_STEP = (UNITS_PER_IMAGE - 1) * PIECES_PER_UNIT + GROUP_LAG + 1
+FIRST_CALL_STEP = PIECES_PER_UNIT + GROUP_LAG + 2
 MULTIPLY_LAG = 1
 STORE_LAG = 2
 LAST_STEP = FIRST_CALL_STEP + (CALLS - 1) * STEPS_PER_CALL + STORE_LAG
@@ -50,16 +44,16 @@ LAST_STEP = FIRST_CALL_STEP + (CALLS - 1) * STEPS_PER_CALL + STORE_LAG
 
 def tile_covpool_k_kernel(tc, x, out):
     nc = tc.nc
-    x_rows = x.rearrange("b c (j h) w -> (b c j) (h w)", j=QUARTERS)
+    x_rows = x.rearrange("b c (j h) w -> (b c j) (h w)", j=2)
 
     with ExitStack() as ctx:
         consts = ctx.enter_context(tc.tile_pool(name="consts", bufs=1))
         resident = ctx.enter_context(tc.tile_pool(name="resident", bufs=1))
-        spread_pool = ctx.enter_context(tc.tile_pool(name="spread", bufs=2))
-        grouped_pool = ctx.enter_context(tc.tile_pool(name="grouped", bufs=2 * BANKS_PER_UNIT))
+        grouped_pool = ctx.enter_context(tc.tile_pool(name="grouped", bufs=2 * PIECES_PER_UNIT))
         mx_pool = ctx.enter_context(tc.tile_pool(name="mx", bufs=3))
         y_pool = ctx.enter_context(tc.tile_pool(name="y", bufs=IMAGES))
-        bank_psum = ctx.enter_context(tc.psum_pool(name="bank_psum", bufs=2 * BANKS_PER_PIECE))
+        spread_pool = ctx.enter_context(tc.tile_pool(name="spread", bufs=2))
+        work_psum = ctx.enter_context(tc.psum_pool(name="work_psum", bufs=2 * BANKS_PER_PIECE))
         stat_psum = ctx.enter_context(tc.psum_pool(name="stat_psum", bufs=1))
         acc_psum = ctx.enter_context(tc.psum_pool(name="acc_psum", bufs=2))
         ctx.enter_context(tc.manual_schedule())
@@ -74,58 +68,60 @@ def tile_covpool_k_kernel(tc, x, out):
 
         ident = consts.tile([P, P], F32)
         make_identity(nc, ident[:])
-        by_mx_word = consts.tile([P, P], F32)
-        nc.vector.tensor_copy(
-            out=by_mx_word[:].rearrange("p (v c j) -> p v c j", v=MX_WORDS_PER_ROW, j=2),
-            in_=ident[:].rearrange("p (c v j) -> p v c j", v=MX_WORDS_PER_ROW, j=2),
+        ident_pairs = ident[:].rearrange("p (c j) -> p c j", j=2)
+        pair_cols = consts.tile([P, P // 2], F32)
+        nc.vector.tensor_tensor(
+            out=pair_cols[:], in0=ident_pairs[:, :, 0], in1=ident_pairs[:, :, 1], op=ALU.add
         )
-        same_channel = consts.tile([P, UNIT_CHANNELS], F32)
-        nc.vector.tensor_reduce(
-            out=same_channel[:],
-            in_=ident[:].rearrange("p (c j) -> p c j", j=QUARTERS),
-            axis=mybir.AxisListType.X,
-            op=ALU.add,
-        )
-        same_channel_bf = consts.tile([P, UNIT_CHANNELS], BF16)
-        nc.vector.tensor_copy(out=same_channel_bf[:], in_=same_channel[:])
-        quarter_mean = consts.tile([P, UNIT_CHANNELS, QUARTERS], F32)
+        pair_cols_bf = consts.tile([P, P // 2], BF16)
+        nc.vector.tensor_copy(out=pair_cols_bf[:], in_=pair_cols[:])
+        one_over_positions = consts.tile([P, 1], F32)
+        nc.vector.memset(one_over_positions[:], 1.0 / POSITIONS)
+        pair_mean = consts.tile([P, P // 2, 2], F32)
         nc.vector.tensor_scalar(
-            out=quarter_mean[:],
-            in0=same_channel[:].unsqueeze(2).to_broadcast([P, UNIT_CHANNELS, QUARTERS]),
+            out=pair_mean[:],
+            in0=pair_cols[:].unsqueeze(2).to_broadcast([P, P // 2, 2]),
             scalar1=1.0 / POSITIONS,
             scalar2=None,
             op0=ALU.mult,
         )
-        one_over_positions = consts.tile([P, 1], F32)
-        nc.vector.memset(one_over_positions[:], 1.0 / POSITIONS)
 
-        vector_sums = resident.tile([P, UNITS], F32)
-        scalar_sums = resident.tile([P, UNITS], F32)
-        means = resident.tile([P, UNITS], F32)
+        vector_sums = [
+            resident.tile([P, PIECES_PER_UNIT], F32, name="vector_sums%d" % u) for u in range(UNITS)
+        ]
+        scalar_sums = [
+            resident.tile([P, PIECES_PER_UNIT], F32, name="scalar_sums%d" % u) for u in range(UNITS)
+        ]
+        means = [resident.tile([P, 1], F32, name="mean%d" % u) for u in range(UNITS)]
         column_sums = {}
         spread_sums = {}
-        mean_psum = {}
         banks = {}
         grouped = {}
         quantised = {}
         acc = {}
 
-        def tensor_add_up(u):
-            sums = stat_psum.tile([P, UNIT_CHANNELS], F32, tag="column_sums")
-            column_sums[u] = sums
+        def piece_of(x_unit, i):
+            return x_unit[:, i * PIECE_COLS : (i + 1) * PIECE_COLS]
+
+        def tensor_add_up(u, i):
+            if i == 0:
+                sums = stat_psum.tile([P, P // 2], F32, tag="column_sums")
+                column_sums[u] = sums
+            piece = piece_of(x_sb[u], i)
             blocks = TENSOR_SUM_COLS // P
             for k in range(blocks):
                 nc.tensor.matmul(
-                    out=sums[:],
-                    lhsT=x_sb[u][:, k * P : (k + 1) * P],
-                    rhs=same_channel_bf[:],
-                    start=(k == 0),
-                    stop=(k == blocks - 1),
+                    out=column_sums[u][:],
+                    lhsT=piece[:, k * P : (k + 1) * P],
+                    rhs=pair_cols_bf[:],
+                    start=(i == 0 and k == 0),
+                    stop=(i == PIECES_PER_UNIT - 1 and k == blocks - 1),
                 )
 
-        def add_up(u):
-            scalar_cols = x_sb[u][:, TENSOR_SUM_COLS : TENSOR_SUM_COLS + SCALAR_SUM_COLS]
-            vector_cols = x_sb[u][:, TENSOR_SUM_COLS + SCALAR_SUM_COLS :]
+        def add_up(u, i):
+            piece = piece_of(x_sb[u], i)
+            vector_cols = piece[:, TENSOR_SUM_COLS : TENSOR_SUM_COLS + VECTOR_SUM_COLS]
+            scalar_cols = piece[:, TENSOR_SUM_COLS + VECTOR_SUM_COLS :]
             nc.vector.tensor_scalar(
                 out=vector_cols,
                 in0=vector_cols,
@@ -133,96 +129,90 @@ def tile_covpool_k_kernel(tc, x, out):
                 scalar2=None,
                 op0=ALU.mult,
                 op1=ALU.add,
-                accum_out=vector_sums[:, u : u + 1],
+                accum_out=vector_sums[u][:, i : i + 1],
             )
             nc.scalar.activation(
-                out=scalar_cols, in_=scalar_cols, func=ACT.Copy, accum_out=scalar_sums[:, u : u + 1]
+                out=scalar_cols,
+                in_=scalar_cols,
+                func=ACT.Copy,
+                accum_out=scalar_sums[u][:, i : i + 1],
             )
 
         def spread(u):
-            repeated = spread_pool.tile([P, UNIT_CHANNELS, QUARTERS], F32, tag="spread")
+            repeated = spread_pool.tile([P, P // 2, 2], F32, tag="spread")
             spread_sums[u] = repeated
             nc.scalar.copy(
-                out=repeated[:],
-                in_=column_sums[u][:].unsqueeze(2).to_broadcast([P, UNIT_CHANNELS, QUARTERS]),
+                out=repeated[:], in_=column_sums[u][:].unsqueeze(2).to_broadcast([P, P // 2, 2])
             )
 
-        def join(u):
-            mean_of_unit = stat_psum.tile([P, 1], F32, tag="mean")
-            mean_psum[u] = mean_of_unit
-            quarters_lhsT = quarter_mean[:].rearrange("p c j -> p (c j)")
+        def join_halves(u):
+            mean_parts = stat_psum.tile([P, PIECES_PER_UNIT + 1], F32, tag="mean_parts")
+            pair_lhsT = pair_mean[:].rearrange("p c j -> p (c j)")
+            by_piece = mean_parts[:, :PIECES_PER_UNIT]
             nc.tensor.matmul(
-                out=mean_of_unit[:],
-                lhsT=quarters_lhsT,
-                rhs=vector_sums[:, u : u + 1],
-                start=True,
-                stop=False,
+                out=by_piece, lhsT=pair_lhsT, rhs=vector_sums[u][:], start=True, stop=False
             )
             nc.tensor.matmul(
-                out=mean_of_unit[:],
-                lhsT=quarters_lhsT,
-                rhs=scalar_sums[:, u : u + 1],
-                start=False,
-                stop=False,
+                out=by_piece, lhsT=pair_lhsT, rhs=scalar_sums[u][:], start=False, stop=True
             )
             nc.tensor.matmul(
-                out=mean_of_unit[:],
+                out=mean_parts[:, PIECES_PER_UNIT:],
                 lhsT=spread_sums[u][:].rearrange("p c j -> p (c j)"),
                 rhs=one_over_positions[:],
-                start=False,
+                start=True,
                 stop=True,
+            )
+            return mean_parts
+
+        def finish_mean(u, mean_parts):
+            nc.vector.tensor_reduce(
+                out=means[u][:], in_=mean_parts[:], axis=mybir.AxisListType.X, op=ALU.add
             )
 
         def centre(u, i):
-            if i == 0:
-                nc.vector.tensor_copy(out=means[:, u : u + 1], in_=mean_psum[u][:])
-            piece = x_sb[u][:, i * PIECE_COLS : (i + 1) * PIECE_COLS]
+            piece = piece_of(x_sb[u], i)
             nc.vector.tensor_scalar(
-                out=piece, in0=piece, scalar1=means[:, u : u + 1], scalar2=None, op0=ALU.subtract
+                out=piece, in0=piece, scalar1=means[u][:, 0:1], scalar2=None, op0=ALU.subtract
             )
 
         def transpose(u, i):
             words = x_sb[u][:].bitcast(F32)
             banks[(u, i)] = []
             for n in range(BANKS_PER_PIECE):
-                bank = bank_psum.tile([P, TRANSPOSES_PER_BANK, P], F32, tag="bank")
+                bank = work_psum.tile([P, TRANSPOSES_PER_BANK, P], F32, tag="work")
                 for t in range(TRANSPOSES_PER_BANK):
                     first = i * PIECE_WORDS + (n * TRANSPOSES_PER_BANK + t) * P
-                    nc.tensor.transpose(bank[:, t, :], words[:, first : first + P], by_mx_word[:])
+                    nc.tensor.transpose(bank[:, t, :], words[:, first : first + P], ident[:])
                 banks[(u, i)].append(bank)
 
         def group(u, i):
-            b, part = divmod(u, UNITS_PER_IMAGE)
-            for n in range(BANKS_PER_PIECE):
-                call = (b, i * BANKS_PER_PIECE + n)
-                if part == 0:
-                    grouped_tile = grouped_pool.tile(
-                        [P, PASSES_PER_BANK * 2 * CHANNELS], F32, tag="grouped", align_bytes=64
-                    )
-                    grouped[call] = grouped_tile
-                by_pass = grouped[call][:].rearrange(
-                    "p (g u w) -> p g u w", g=PASSES_PER_BANK, u=UNITS_PER_IMAGE
+            b, r = divmod(u, 2)
+            if r == 0:
+                grouped_tile = grouped_pool.tile(
+                    [P, 2 * PIECE_WORDS], F32, tag="grouped", align_bytes=64
                 )
-                nc.scalar.copy(
-                    out=by_pass[:, :, part, :],
-                    in_=banks[(u, i)][n][:].rearrange("p t (v w) -> p (t v) w", v=MX_WORDS_PER_ROW),
-                )
-
-        def quantise(call):
-            codes = mx_pool.tile([P, PASSES_PER_BANK * CHANNELS], U32, tag="codes", align_bytes=64)
-            scales = mx_pool.tile([P, PASSES_PER_BANK * CHANNELS], U8, tag="scales", align_bytes=64)
-            nc.vector.quantize_mx(
-                out=codes[:].bitcast(FP8X4), scales=scales[:], in_=grouped[call][:].bitcast(BF16)
+                grouped[(b, i)] = grouped_tile
+            by_pass = grouped[(b, i)][:].rearrange(
+                "p (g r w) -> p g r w", g=PASSES_PER_PIECE, r=2
             )
-            quantised[call] = (codes, scales)
+            for n in range(BANKS_PER_PIECE):
+                passes = slice(n * TRANSPOSES_PER_BANK, (n + 1) * TRANSPOSES_PER_BANK)
+                nc.scalar.copy(out=by_pass[:, passes, r, :], in_=banks[(u, i)][n][:])
 
-        def multiply(call):
-            b, n = call
-            if n == 0:
+        def quantise(b, i):
+            codes = mx_pool.tile([P, PASSES_PER_PIECE * CHANNELS], U32, tag="codes", align_bytes=64)
+            scales = mx_pool.tile([P, PASSES_PER_PIECE * CHANNELS], U8, tag="scales", align_bytes=64)
+            nc.vector.quantize_mx(
+                out=codes[:].bitcast(FP8X4), scales=scales[:], in_=grouped[(b, i)][:].bitcast(BF16)
+            )
+            quantised[(b, i)] = (codes, scales)
+
+        def multiply(b, i):
+            if i == 0:
                 acc_tile = acc_psum.tile([CHANNELS, CHANNELS], F32, tag="acc")
                 acc[b] = acc_tile
-            codes, scales = quantised[call]
-            for g in range(PASSES_PER_BANK):
+            codes, scales = quantised[(b, i)]
+            for g in range(PASSES_PER_PIECE):
                 cols = slice(g * CHANNELS, (g + 1) * CHANNELS)
                 nc.tensor.matmul_mx(
                     out=acc[b][:],
@@ -230,8 +220,8 @@ def tile_covpool_k_kernel(tc, x, out):
                     lhsT_scale=scales[:, cols],
                     rhs=codes[:, cols].bitcast(FP8X4),
                     rhs_scale=scales[:, cols],
-                    start=(n == 0 and g == 0),
-                    stop=(n == BANKS_PER_UNIT - 1 and g == PASSES_PER_BANK - 1),
+                    start=(i == 0 and g == 0),
+                    stop=(i == PIECES_PER_UNIT - 1 and g == PASSES_PER_PIECE - 1),
                 )
 
         def store(b):
@@ -247,23 +237,24 @@ def tile_covpool_k_kernel(tc, x, out):
         def call_at(s, lag):
             steps = s - lag - FIRST_CALL_STEP
             if steps >= 0 and steps % STEPS_PER_CALL == 0 and steps // STEPS_PER_CALL < CALLS:
-                return divmod(steps // STEPS_PER_CALL, BANKS_PER_UNIT)
+                return divmod(steps // STEPS_PER_CALL, PIECES_PER_UNIT)
             return None
 
-        first_piece = 0
-        last_piece = PIECES_PER_UNIT - 1
+        mean_parts_of = {}
         for s in range(LAST_STEP + 1):
             to_quantise = call_at(s, 0)
             if to_quantise is not None:
-                quantise(to_quantise)
+                quantise(to_quantise[0], to_quantise[1])
             to_spread = piece_at(s, SPREAD_LAG)
-            if to_spread is not None and to_spread[1] == first_piece:
+            if to_spread is not None and to_spread[1] == PIECES_PER_UNIT - 1:
                 spread(to_spread[0])
             to_join = piece_at(s, JOIN_LAG)
-            if to_join is not None and to_join[1] == last_piece:
-                join(to_join[0])
+            if to_join is not None and to_join[1] == PIECES_PER_UNIT - 1:
+                mean_parts_of[to_join[0]] = join_halves(to_join[0])
             to_centre = piece_at(s, CENTRE_LAG)
             if to_centre is not None:
+                if to_centre[1] == 0:
+                    finish_mean(to_centre[0], mean_parts_of[to_centre[0]])
                 centre(to_centre[0], to_centre[1])
             to_transpose = piece_at(s, TRANSPOSE_LAG)
             if to_transpose is not None:
@@ -273,12 +264,11 @@ def tile_covpool_k_kernel(tc, x, out):
                 group(to_group[0], to_group[1])
             to_multiply = call_at(s, MULTIPLY_LAG)
             if to_multiply is not None:
-                multiply(to_multiply)
+                multiply(to_multiply[0], to_multiply[1])
             to_store = call_at(s, STORE_LAG)
-            if to_store is not None and to_store[1] == BANKS_PER_UNIT - 1:
+            if to_store is not None and to_store[1] == PIECES_PER_UNIT - 1:
                 store(to_store[0])
-            loaded = piece_at(s, 0)
-            if loaded is not None and loaded[1] == first_piece:
-                tensor_add_up(loaded[0])
-            if loaded is not None and loaded[1] == last_piece:
-                add_up(loaded[0])
+            to_add_up = piece_at(s, 0)
+            if to_add_up is not None:
+                tensor_add_up(to_add_up[0], to_add_up[1])
+                add_up(to_add_up[0], to_add_up[1])

@@ -10,6 +10,7 @@ U8 = mybir.dt.uint8
 FP8X4 = mybir.dt.float8_e4m3fn_x4
 ALU = mybir.AluOpType
 ACT = mybir.ActivationFunctionType
+AXIS = mybir.AxisListType
 
 IMAGES = 4
 CHANNELS = 128
@@ -17,44 +18,65 @@ POSITIONS = 16384
 FLOPS = 2 * IMAGES * CHANNELS * CHANNELS * POSITIONS
 
 P = 128
-UNITS = 2 * IMAGES
-UNIT_COLS = POSITIONS // 2
-PIECES_PER_UNIT = 4
+PARTS = 4
+UNIT_CHANNELS = P // PARTS
+UNITS_PER_IMAGE = CHANNELS // UNIT_CHANNELS
+UNITS = IMAGES * UNITS_PER_IMAGE
+UNIT_COLS = POSITIONS // PARTS
+PIECE_COLS = 2048
+PIECES_PER_UNIT = UNIT_COLS // PIECE_COLS
+PIECES_PER_IMAGE = UNITS_PER_IMAGE * PIECES_PER_UNIT
 PIECES = UNITS * PIECES_PER_UNIT
-PIECE_COLS = UNIT_COLS // PIECES_PER_UNIT
-PIECE_WORDS = PIECE_COLS // 2
-BANK_WORDS = 512
-TRANSPOSES_PER_BANK = BANK_WORDS // P
-BANKS_PER_PIECE = PIECE_WORDS // BANK_WORDS
-PASSES_PER_PIECE = PIECE_WORDS // P
-TENSOR_SUM_COLS = 384
-VECTOR_SUM_COLS = 1152
+STRETCHES_PER_BANK = 2
+BANKS_PER_PIECE = PIECE_COLS // (512 * STRETCHES_PER_BANK)
+PASSES_PER_PIECE = PARTS * PIECE_COLS // 512
+PASSES_PER_CALL = 8
+CALLS_PER_PIECE = PASSES_PER_PIECE // PASSES_PER_CALL
+CALLS_PER_IMAGE = PIECES_PER_UNIT * CALLS_PER_PIECE
+TENSOR_COLS = (0, 384, 1280, 1280)
+VECTOR_COLS = (1216, 1408, 512, 512)
+
+
+def tensor_cols(u):
+    return TENSOR_COLS[u // UNITS_PER_IMAGE]
+
+
+def vector_cols(u):
+    return VECTOR_COLS[u // UNITS_PER_IMAGE]
+
+
+def scalar_cols(u):
+    return PIECE_COLS - tensor_cols(u) - vector_cols(u)
+
+
+def adders(u):
+    return 2 if scalar_cols(u) else 1
+
+
 SPREAD_LAG = 1
 JOIN_LAG = 2
-CENTRE_LAG = PIECES_PER_UNIT + 2
+CENTRE_LAG = PIECES_PER_UNIT + 3
 TRANSPOSE_LAG = CENTRE_LAG + 1
 GROUP_LAG = CENTRE_LAG + 2
-CALLS = IMAGES * PIECES_PER_UNIT
-STEPS_PER_CALL = PIECES // CALLS
-FIRST_CALL_STEP = PIECES_PER_UNIT + GROUP_LAG + 2
+CALL_GAP = 2
+CALL_LAG = 2
 MULTIPLY_LAG = 1
 STORE_LAG = 2
-LAST_STEP = FIRST_CALL_STEP + (CALLS - 1) * STEPS_PER_CALL + STORE_LAG
 
 
 def tile_covpool_k_kernel(tc, x, out):
     nc = tc.nc
-    x_rows = x.rearrange("b c (j h) w -> (b c j) (h w)", j=2)
+    x_rows = x.rearrange("b c (j h) w -> (b c j) (h w)", j=PARTS)
 
     with ExitStack() as ctx:
         consts = ctx.enter_context(tc.tile_pool(name="consts", bufs=1))
         resident = ctx.enter_context(tc.tile_pool(name="resident", bufs=1))
         grouped_pool = ctx.enter_context(tc.tile_pool(name="grouped", bufs=2 * PIECES_PER_UNIT))
         mx_pool = ctx.enter_context(tc.tile_pool(name="mx", bufs=3))
-        y_pool = ctx.enter_context(tc.tile_pool(name="y", bufs=IMAGES))
-        spread_pool = ctx.enter_context(tc.tile_pool(name="spread", bufs=2))
-        work_psum = ctx.enter_context(tc.psum_pool(name="work_psum", bufs=2 * BANKS_PER_PIECE))
-        stat_psum = ctx.enter_context(tc.psum_pool(name="stat_psum", bufs=1))
+        small = ctx.enter_context(tc.tile_pool(name="small", bufs=4))
+        work_psum = ctx.enter_context(tc.psum_pool(name="work_psum", bufs=4))
+        sums_psum = ctx.enter_context(tc.psum_pool(name="sums_psum", bufs=1))
+        mean_psum = ctx.enter_context(tc.psum_pool(name="mean_psum", bufs=1))
         acc_psum = ctx.enter_context(tc.psum_pool(name="acc_psum", bufs=2))
         ctx.enter_context(tc.manual_schedule())
 
@@ -66,31 +88,36 @@ def tile_covpool_k_kernel(tc, x, out):
                 cols = slice(i * PIECE_COLS, (i + 1) * PIECE_COLS)
                 nc.sync.dma_start(out=x_unit[:, cols], in_=x_rows[u * P : (u + 1) * P, cols])
 
-        ident = consts.tile([P, P], F32)
-        make_identity(nc, ident[:])
-        ident_pairs = ident[:].rearrange("p (c j) -> p c j", j=2)
-        pair_cols = consts.tile([P, P // 2], F32)
-        nc.vector.tensor_tensor(
-            out=pair_cols[:], in0=ident_pairs[:, :, 0], in1=ident_pairs[:, :, 1], op=ALU.add
-        )
-        pair_cols_bf = consts.tile([P, P // 2], BF16)
-        nc.vector.tensor_copy(out=pair_cols_bf[:], in_=pair_cols[:])
         one_over_positions = consts.tile([P, 1], F32)
         nc.vector.memset(one_over_positions[:], 1.0 / POSITIONS)
-        pair_mean = consts.tile([P, P // 2, 2], F32)
+        first_copy = consts.tile([P, 1], F32)
+        nc.scalar.activation(out=first_copy[:], in_=one_over_positions[:], func=ACT.Copy)
+        ident = consts.tile([P, P], F32)
+        make_identity(nc, ident[:])
+        own_channel = consts.tile([P, UNIT_CHANNELS], F32)
+        nc.vector.tensor_reduce(
+            out=own_channel[:],
+            in_=ident[:].rearrange("q (c j) -> q c j", j=PARTS),
+            axis=AXIS.X,
+            op=ALU.add,
+        )
+        own_channel_bf = consts.tile([P, UNIT_CHANNELS], BF16)
+        nc.vector.tensor_copy(out=own_channel_bf[:], in_=own_channel[:])
+        part_averaging = consts.tile([P, UNIT_CHANNELS, PARTS], F32)
         nc.vector.tensor_scalar(
-            out=pair_mean[:],
-            in0=pair_cols[:].unsqueeze(2).to_broadcast([P, P // 2, 2]),
+            out=part_averaging[:],
+            in0=own_channel[:].unsqueeze(2).to_broadcast([P, UNIT_CHANNELS, PARTS]),
             scalar1=1.0 / POSITIONS,
             scalar2=None,
             op0=ALU.mult,
         )
+        ident_by_part = consts.tile([P, PARTS, UNIT_CHANNELS], F32)
+        nc.vector.tensor_copy(
+            out=ident_by_part[:], in_=ident[:].rearrange("q (c j) -> q j c", j=PARTS)
+        )
 
-        vector_sums = [
-            resident.tile([P, PIECES_PER_UNIT], F32, name="vector_sums%d" % u) for u in range(UNITS)
-        ]
-        scalar_sums = [
-            resident.tile([P, PIECES_PER_UNIT], F32, name="scalar_sums%d" % u) for u in range(UNITS)
+        addends = [
+            resident.tile([P, adders(u) * PIECES_PER_UNIT], F32, name="addends%d" % u) for u in range(UNITS)
         ]
         means = [resident.tile([P, 1], F32, name="mean%d" % u) for u in range(UNITS)]
         column_sums = {}
@@ -100,77 +127,86 @@ def tile_covpool_k_kernel(tc, x, out):
         quantised = {}
         acc = {}
 
-        def piece_of(x_unit, i):
-            return x_unit[:, i * PIECE_COLS : (i + 1) * PIECE_COLS]
+        def piece_of(u, i):
+            return x_sb[u][:, i * PIECE_COLS : (i + 1) * PIECE_COLS]
 
         def tensor_add_up(u, i):
+            if tensor_cols(u) == 0:
+                return
             if i == 0:
-                sums = stat_psum.tile([P, P // 2], F32, tag="column_sums")
+                sums = sums_psum.tile([P, UNIT_CHANNELS], F32, tag="column_sums")
                 column_sums[u] = sums
-            piece = piece_of(x_sb[u], i)
-            blocks = TENSOR_SUM_COLS // P
+            piece = piece_of(u, i)
+            blocks = tensor_cols(u) // P
             for k in range(blocks):
                 nc.tensor.matmul(
                     out=column_sums[u][:],
                     lhsT=piece[:, k * P : (k + 1) * P],
-                    rhs=pair_cols_bf[:],
+                    rhs=own_channel_bf[:],
                     start=(i == 0 and k == 0),
                     stop=(i == PIECES_PER_UNIT - 1 and k == blocks - 1),
                 )
 
         def add_up(u, i):
-            piece = piece_of(x_sb[u], i)
-            vector_cols = piece[:, TENSOR_SUM_COLS : TENSOR_SUM_COLS + VECTOR_SUM_COLS]
-            scalar_cols = piece[:, TENSOR_SUM_COLS + VECTOR_SUM_COLS :]
+            piece = piece_of(u, i)
+            first = tensor_cols(u)
+            cols_v = piece[:, first : first + vector_cols(u)]
+            cols_s = piece[:, first + vector_cols(u) :]
+            a = adders(u)
             nc.vector.tensor_scalar(
-                out=vector_cols,
-                in0=vector_cols,
+                out=cols_v,
+                in0=cols_v,
                 scalar1=1.0,
                 scalar2=None,
                 op0=ALU.mult,
                 op1=ALU.add,
-                accum_out=vector_sums[u][:, i : i + 1],
+                accum_out=addends[u][:, a * i : a * i + 1],
             )
-            nc.scalar.activation(
-                out=scalar_cols,
-                in_=scalar_cols,
-                func=ACT.Copy,
-                accum_out=scalar_sums[u][:, i : i + 1],
-            )
+            if a == 2:
+                nc.scalar.activation(
+                    out=cols_s,
+                    in_=cols_s,
+                    func=ACT.Copy,
+                    accum_out=addends[u][:, a * i + 1 : a * i + 2],
+                )
 
         def spread(u):
-            repeated = spread_pool.tile([P, P // 2, 2], F32, tag="spread")
+            if tensor_cols(u) == 0:
+                return
+            repeated = small.tile([P, UNIT_CHANNELS, PARTS], F32, tag="spread")
             spread_sums[u] = repeated
             nc.scalar.copy(
-                out=repeated[:], in_=column_sums[u][:].unsqueeze(2).to_broadcast([P, P // 2, 2])
+                out=repeated[:],
+                in_=column_sums[u][:].unsqueeze(2).to_broadcast([P, UNIT_CHANNELS, PARTS]),
             )
 
-        def join_halves(u):
-            mean_parts = stat_psum.tile([P, PIECES_PER_UNIT + 1], F32, tag="mean_parts")
-            pair_lhsT = pair_mean[:].rearrange("p c j -> p (c j)")
-            by_piece = mean_parts[:, :PIECES_PER_UNIT]
+        def join(u):
+            parts = adders(u) * PIECES_PER_UNIT
+            if tensor_cols(u):
+                parts += 1
+            mean_parts = mean_psum.tile([P, parts], F32, tag="mean_parts")
             nc.tensor.matmul(
-                out=by_piece, lhsT=pair_lhsT, rhs=vector_sums[u][:], start=True, stop=False
-            )
-            nc.tensor.matmul(
-                out=by_piece, lhsT=pair_lhsT, rhs=scalar_sums[u][:], start=False, stop=True
-            )
-            nc.tensor.matmul(
-                out=mean_parts[:, PIECES_PER_UNIT:],
-                lhsT=spread_sums[u][:].rearrange("p c j -> p (c j)"),
-                rhs=one_over_positions[:],
+                out=mean_parts[:, : adders(u) * PIECES_PER_UNIT],
+                lhsT=part_averaging[:].rearrange("p c j -> p (c j)"),
+                rhs=addends[u][:],
                 start=True,
                 stop=True,
             )
+            if tensor_cols(u):
+                nc.tensor.matmul(
+                    out=mean_parts[:, parts - 1 :],
+                    lhsT=spread_sums[u][:].rearrange("p c j -> p (c j)"),
+                    rhs=one_over_positions[:],
+                    start=True,
+                    stop=True,
+                )
             return mean_parts
 
         def finish_mean(u, mean_parts):
-            nc.vector.tensor_reduce(
-                out=means[u][:], in_=mean_parts[:], axis=mybir.AxisListType.X, op=ALU.add
-            )
+            nc.vector.tensor_reduce(out=means[u][:], in_=mean_parts[:], axis=AXIS.X, op=ALU.add)
 
         def centre(u, i):
-            piece = piece_of(x_sb[u], i)
+            piece = piece_of(u, i)
             nc.vector.tensor_scalar(
                 out=piece, in0=piece, scalar1=means[u][:, 0:1], scalar2=None, op0=ALU.subtract
             )
@@ -179,40 +215,55 @@ def tile_covpool_k_kernel(tc, x, out):
             words = x_sb[u][:].bitcast(F32)
             banks[(u, i)] = []
             for n in range(BANKS_PER_PIECE):
-                bank = work_psum.tile([P, TRANSPOSES_PER_BANK, P], F32, tag="work")
-                for t in range(TRANSPOSES_PER_BANK):
-                    first = i * PIECE_WORDS + (n * TRANSPOSES_PER_BANK + t) * P
-                    nc.tensor.transpose(bank[:, t, :], words[:, first : first + P], ident[:])
+                bank = work_psum.tile(
+                    [P, PARTS, STRETCHES_PER_BANK, 2, UNIT_CHANNELS], F32, tag="work"
+                )
+                for s in range(STRETCHES_PER_BANK):
+                    for h in range(2):
+                        stretch = (i * BANKS_PER_PIECE + n) * STRETCHES_PER_BANK + s
+                        first = (2 * stretch + h) * P
+                        nc.tensor.transpose(
+                            bank[:, :, s, h, :],
+                            words[:, first : first + P],
+                            ident_by_part[:].rearrange("q j c -> q (j c)"),
+                        )
                 banks[(u, i)].append(bank)
 
         def group(u, i):
-            b, r = divmod(u, 2)
+            b, r = divmod(u, UNITS_PER_IMAGE)
             if r == 0:
                 grouped_tile = grouped_pool.tile(
-                    [P, 2 * PIECE_WORDS], F32, tag="grouped", align_bytes=64
+                    [P, BANKS_PER_PIECE, PARTS * STRETCHES_PER_BANK, CHANNELS, 2],
+                    F32,
+                    tag="grouped",
+                    align_bytes=64,
                 )
                 grouped[(b, i)] = grouped_tile
-            by_pass = grouped[(b, i)][:].rearrange(
-                "p (g r w) -> p g r w", g=PASSES_PER_PIECE, r=2
-            )
             for n in range(BANKS_PER_PIECE):
-                passes = slice(n * TRANSPOSES_PER_BANK, (n + 1) * TRANSPOSES_PER_BANK)
-                nc.scalar.copy(out=by_pass[:, passes, r, :], in_=banks[(u, i)][n][:])
+                nc.scalar.copy(
+                    out=grouped[(b, i)][:, n, :, r * UNIT_CHANNELS : (r + 1) * UNIT_CHANNELS, :],
+                    in_=banks[(u, i)][n][:].rearrange("p j s h c -> p (j s) c h"),
+                )
 
-        def quantise(b, i):
-            codes = mx_pool.tile([P, PASSES_PER_PIECE * CHANNELS], U32, tag="codes", align_bytes=64)
-            scales = mx_pool.tile([P, PASSES_PER_PIECE * CHANNELS], U8, tag="scales", align_bytes=64)
+        def quantise(b, k):
+            i, part_call = divmod(k, CALLS_PER_PIECE)
+            codes = mx_pool.tile([P, PASSES_PER_CALL * CHANNELS], U32, tag="codes", align_bytes=64)
+            scales = mx_pool.tile([P, PASSES_PER_CALL * CHANNELS], U8, tag="scales", align_bytes=64)
+            words = grouped[(b, i)][:].rearrange("p n g c h -> p (n g c h)")
+            width = PASSES_PER_CALL * CHANNELS * 2
             nc.vector.quantize_mx(
-                out=codes[:].bitcast(FP8X4), scales=scales[:], in_=grouped[(b, i)][:].bitcast(BF16)
+                out=codes[:].bitcast(FP8X4),
+                scales=scales[:],
+                in_=words[:, part_call * width : (part_call + 1) * width].bitcast(BF16),
             )
-            quantised[(b, i)] = (codes, scales)
+            quantised[(b, k)] = (codes, scales)
 
-        def multiply(b, i):
-            if i == 0:
+        def multiply(b, k):
+            if k == 0:
                 acc_tile = acc_psum.tile([CHANNELS, CHANNELS], F32, tag="acc")
                 acc[b] = acc_tile
-            codes, scales = quantised[(b, i)]
-            for g in range(PASSES_PER_PIECE):
+            codes, scales = quantised[(b, k)]
+            for g in range(PASSES_PER_CALL):
                 cols = slice(g * CHANNELS, (g + 1) * CHANNELS)
                 nc.tensor.matmul_mx(
                     out=acc[b][:],
@@ -220,12 +271,12 @@ def tile_covpool_k_kernel(tc, x, out):
                     lhsT_scale=scales[:, cols],
                     rhs=codes[:, cols].bitcast(FP8X4),
                     rhs_scale=scales[:, cols],
-                    start=(i == 0 and g == 0),
-                    stop=(i == PIECES_PER_UNIT - 1 and g == PASSES_PER_PIECE - 1),
+                    start=(k == 0 and g == 0),
+                    stop=(k == CALLS_PER_IMAGE - 1 and g == PASSES_PER_CALL - 1),
                 )
 
         def store(b):
-            y_sb = y_pool.tile([CHANNELS, CHANNELS], F32, tag="y")
+            y_sb = small.tile([CHANNELS, CHANNELS], F32, tag="y")
             nc.scalar.activation(out=y_sb[:], in_=acc[b][:], func=ACT.Copy, scale=1.0 / POSITIONS)
             nc.sync.dma_start(out=out[b], in_=y_sb[:])
 
@@ -234,14 +285,21 @@ def tile_covpool_k_kernel(tc, x, out):
                 return divmod(s - lag, PIECES_PER_UNIT)
             return None
 
+        call_step = {}
+        step = 0
+        for b in range(IMAGES):
+            for k in range(CALLS_PER_IMAGE):
+                last_piece = (b + 1) * PIECES_PER_IMAGE - PIECES_PER_UNIT + k // CALLS_PER_PIECE
+                step = max(step, last_piece + GROUP_LAG + CALL_LAG)
+                call_step[step] = (b, k)
+                step += CALL_GAP if step < PIECES else 1
+        last_step = max(call_step) + STORE_LAG
+
         def call_at(s, lag):
-            steps = s - lag - FIRST_CALL_STEP
-            if steps >= 0 and steps % STEPS_PER_CALL == 0 and steps // STEPS_PER_CALL < CALLS:
-                return divmod(steps // STEPS_PER_CALL, PIECES_PER_UNIT)
-            return None
+            return call_step.get(s - lag)
 
         mean_parts_of = {}
-        for s in range(LAST_STEP + 1):
+        for s in range(last_step + 1):
             to_quantise = call_at(s, 0)
             if to_quantise is not None:
                 quantise(to_quantise[0], to_quantise[1])
@@ -250,12 +308,13 @@ def tile_covpool_k_kernel(tc, x, out):
                 spread(to_spread[0])
             to_join = piece_at(s, JOIN_LAG)
             if to_join is not None and to_join[1] == PIECES_PER_UNIT - 1:
-                mean_parts_of[to_join[0]] = join_halves(to_join[0])
+                mean_parts_of[to_join[0]] = join(to_join[0])
             to_centre = piece_at(s, CENTRE_LAG)
             if to_centre is not None:
-                if to_centre[1] == 0:
-                    finish_mean(to_centre[0], mean_parts_of[to_centre[0]])
                 centre(to_centre[0], to_centre[1])
+            to_finish = piece_at(s, CENTRE_LAG - 1)
+            if to_finish is not None and to_finish[1] == 0:
+                finish_mean(to_finish[0], mean_parts_of[to_finish[0]])
             to_transpose = piece_at(s, TRANSPOSE_LAG)
             if to_transpose is not None:
                 transpose(to_transpose[0], to_transpose[1])
@@ -266,7 +325,7 @@ def tile_covpool_k_kernel(tc, x, out):
             if to_multiply is not None:
                 multiply(to_multiply[0], to_multiply[1])
             to_store = call_at(s, STORE_LAG)
-            if to_store is not None and to_store[1] == PIECES_PER_UNIT - 1:
+            if to_store is not None and to_store[1] == CALLS_PER_IMAGE - 1:
                 store(to_store[0])
             to_add_up = piece_at(s, 0)
             if to_add_up is not None:

@@ -33,8 +33,8 @@ PASSES_PER_PIECE = PARTS * PIECE_COLS // 512
 PASSES_PER_CALL = 8
 CALLS_PER_PIECE = PASSES_PER_PIECE // PASSES_PER_CALL
 CALLS_PER_IMAGE = PIECES_PER_UNIT * CALLS_PER_PIECE
-TENSOR_COLS = (0, 384, 1280, 1280)
-VECTOR_COLS = (1216, 1408, 512, 512)
+TENSOR_COLS = (0, 256, 1280, 1280)
+VECTOR_COLS = (1216, 1536, 512, 512)
 
 
 def tensor_cols(u):
@@ -49,19 +49,26 @@ def scalar_cols(u):
     return PIECE_COLS - tensor_cols(u) - vector_cols(u)
 
 
+WHOLE = (False, True, True, True)
+
+
+def addends_of(u):
+    return adders(u) * (1 if WHOLE[u // UNITS_PER_IMAGE] else PIECES_PER_UNIT)
+
+
 def adders(u):
     return 2 if scalar_cols(u) else 1
 
 
 SPREAD_LAG = 1
 JOIN_LAG = 2
-CENTRE_LAG = PIECES_PER_UNIT + 3
-TRANSPOSE_LAG = CENTRE_LAG + 1
-GROUP_LAG = CENTRE_LAG + 2
 CALL_GAP = 2
 CALL_LAG = 2
 MULTIPLY_LAG = 1
-STORE_LAG = 2
+MEAN_LAG = 4
+ORDER = list(range(PIECES - 4)) + [PIECES - 4, PIECES - 2, PIECES - 3, PIECES - 1]
+TR_LAG = 1
+GR_LAG = 2
 
 
 def tile_covpool_k_kernel(tc, x, out):
@@ -72,7 +79,7 @@ def tile_covpool_k_kernel(tc, x, out):
         consts = ctx.enter_context(tc.tile_pool(name="consts", bufs=1))
         resident = ctx.enter_context(tc.tile_pool(name="resident", bufs=1))
         grouped_pool = ctx.enter_context(tc.tile_pool(name="grouped", bufs=2 * PIECES_PER_UNIT))
-        mx_pool = ctx.enter_context(tc.tile_pool(name="mx", bufs=3))
+        mx_pool = ctx.enter_context(tc.tile_pool(name="mx", bufs=6))
         small = ctx.enter_context(tc.tile_pool(name="small", bufs=4))
         work_psum = ctx.enter_context(tc.psum_pool(name="work_psum", bufs=4))
         sums_psum = ctx.enter_context(tc.psum_pool(name="sums_psum", bufs=1))
@@ -117,7 +124,7 @@ def tile_covpool_k_kernel(tc, x, out):
         )
 
         addends = [
-            resident.tile([P, adders(u) * PIECES_PER_UNIT], F32, name="addends%d" % u) for u in range(UNITS)
+            resident.tile([P, addends_of(u)], F32, name="addends%d" % u) for u in range(UNITS)
         ]
         means = [resident.tile([P, 1], F32, name="mean%d" % u) for u in range(UNITS)]
         column_sums = {}
@@ -148,10 +155,18 @@ def tile_covpool_k_kernel(tc, x, out):
                 )
 
         def add_up(u, i):
-            piece = piece_of(u, i)
             first = tensor_cols(u)
-            cols_v = piece[:, first : first + vector_cols(u)]
-            cols_s = piece[:, first + vector_cols(u) :]
+            if WHOLE[u // UNITS_PER_IMAGE]:
+                if i < PIECES_PER_UNIT - 1:
+                    return
+                piece = x_sb[u][:].rearrange("p (i n) -> p i n", i=PIECES_PER_UNIT)
+                cols_v = piece[:, :, first : first + vector_cols(u)]
+                cols_s = piece[:, :, first + vector_cols(u) :]
+                i = 0
+            else:
+                piece = piece_of(u, i)
+                cols_v = piece[:, first : first + vector_cols(u)]
+                cols_s = piece[:, first + vector_cols(u) :]
             a = adders(u)
             nc.vector.tensor_scalar(
                 out=cols_v,
@@ -181,12 +196,12 @@ def tile_covpool_k_kernel(tc, x, out):
             )
 
         def join(u):
-            parts = adders(u) * PIECES_PER_UNIT
+            parts = addends_of(u)
             if tensor_cols(u):
                 parts += 1
             mean_parts = mean_psum.tile([P, parts], F32, tag="mean_parts")
             nc.tensor.matmul(
-                out=mean_parts[:, : adders(u) * PIECES_PER_UNIT],
+                out=mean_parts[:, : addends_of(u)],
                 lhsT=part_averaging[:].rearrange("p c j -> p (c j)"),
                 rhs=addends[u][:],
                 start=True,
@@ -231,7 +246,7 @@ def tile_covpool_k_kernel(tc, x, out):
 
         def group(u, i):
             b, r = divmod(u, UNITS_PER_IMAGE)
-            if r == 0:
+            if (b, i) not in grouped:
                 grouped_tile = grouped_pool.tile(
                     [P, BANKS_PER_PIECE, PARTS * STRETCHES_PER_BANK, CHANNELS, 2],
                     F32,
@@ -280,54 +295,63 @@ def tile_covpool_k_kernel(tc, x, out):
             nc.scalar.activation(out=y_sb[:], in_=acc[b][:], func=ACT.Copy, scale=1.0 / POSITIONS)
             nc.sync.dma_start(out=out[b], in_=y_sb[:])
 
-        def piece_at(s, lag):
-            if 0 <= s - lag < PIECES:
-                return divmod(s - lag, PIECES_PER_UNIT)
-            return None
-
+        to_spread, to_join, to_finish = {}, {}, {}
+        to_centre, to_transpose, to_group, group_step = {}, {}, {}, {}
+        mean_step = {}
+        for u in range(UNITS):
+            end = (u + 1) * PIECES_PER_UNIT - 1
+            to_spread.setdefault(end + SPREAD_LAG, []).append(u)
+            to_join.setdefault(end + JOIN_LAG, []).append(u)
+            to_finish.setdefault(end + MEAN_LAG - 1, []).append(u)
+            mean_step[u] = end + MEAN_LAG
+        step = 0
+        for p in ORDER:
+            step = max(step, mean_step[p // PIECES_PER_UNIT])
+            to_centre[step] = p
+            to_transpose[step + TR_LAG] = p
+            to_group[step + GR_LAG] = p
+            group_step[p] = step + GR_LAG
+            step += 1
         call_step = {}
         step = 0
         for b in range(IMAGES):
             for k in range(CALLS_PER_IMAGE):
-                last_piece = (b + 1) * PIECES_PER_IMAGE - PIECES_PER_UNIT + k // CALLS_PER_PIECE
-                step = max(step, last_piece + GROUP_LAG + CALL_LAG)
+                i = k // CALLS_PER_PIECE
+                ready = max(
+                    group_step[b * PIECES_PER_IMAGE + r * PIECES_PER_UNIT + i]
+                    for r in range(UNITS_PER_IMAGE)
+                )
+                step = max(step, ready + CALL_LAG)
                 call_step[step] = (b, k)
                 step += CALL_GAP if step < PIECES else 1
-        last_step = max(call_step) + STORE_LAG
-
-        def call_at(s, lag):
-            return call_step.get(s - lag)
+        multiply_at = {}
+        step = 0
+        for s in sorted(call_step):
+            step = max(step, s + MULTIPLY_LAG)
+            multiply_at.setdefault(step, []).append(call_step[s])
+        last_step = max(multiply_at) + 1
 
         mean_parts_of = {}
         for s in range(last_step + 1):
-            to_quantise = call_at(s, 0)
-            if to_quantise is not None:
-                quantise(to_quantise[0], to_quantise[1])
-            to_spread = piece_at(s, SPREAD_LAG)
-            if to_spread is not None and to_spread[1] == PIECES_PER_UNIT - 1:
-                spread(to_spread[0])
-            to_join = piece_at(s, JOIN_LAG)
-            if to_join is not None and to_join[1] == PIECES_PER_UNIT - 1:
-                mean_parts_of[to_join[0]] = join(to_join[0])
-            to_centre = piece_at(s, CENTRE_LAG)
-            if to_centre is not None:
-                centre(to_centre[0], to_centre[1])
-            to_finish = piece_at(s, CENTRE_LAG - 1)
-            if to_finish is not None and to_finish[1] == 0:
-                finish_mean(to_finish[0], mean_parts_of[to_finish[0]])
-            to_transpose = piece_at(s, TRANSPOSE_LAG)
-            if to_transpose is not None:
-                transpose(to_transpose[0], to_transpose[1])
-            to_group = piece_at(s, GROUP_LAG)
-            if to_group is not None:
-                group(to_group[0], to_group[1])
-            to_multiply = call_at(s, MULTIPLY_LAG)
-            if to_multiply is not None:
-                multiply(to_multiply[0], to_multiply[1])
-            to_store = call_at(s, STORE_LAG)
-            if to_store is not None and to_store[1] == CALLS_PER_IMAGE - 1:
-                store(to_store[0])
-            to_add_up = piece_at(s, 0)
-            if to_add_up is not None:
-                tensor_add_up(to_add_up[0], to_add_up[1])
-                add_up(to_add_up[0], to_add_up[1])
+            if s in call_step:
+                quantise(call_step[s][0], call_step[s][1])
+            for u in to_spread.get(s, []):
+                spread(u)
+            for u in to_join.get(s, []):
+                mean_parts_of[u] = join(u)
+            if s in to_centre:
+                centre(*divmod(to_centre[s], PIECES_PER_UNIT))
+            for u in to_finish.get(s, []):
+                finish_mean(u, mean_parts_of[u])
+            if s in to_transpose:
+                transpose(*divmod(to_transpose[s], PIECES_PER_UNIT))
+            if s in to_group:
+                group(*divmod(to_group[s], PIECES_PER_UNIT))
+            for call in multiply_at.get(s, []):
+                multiply(call[0], call[1])
+            for call in multiply_at.get(s - 1, []):
+                if call[1] == CALLS_PER_IMAGE - 1:
+                    store(call[0])
+            if s < PIECES:
+                tensor_add_up(*divmod(s, PIECES_PER_UNIT))
+                add_up(*divmod(s, PIECES_PER_UNIT))

@@ -266,11 +266,17 @@ def tile_covpool_k_kernel(tc, x, out):
             scales = mx_pool.tile([P, PASSES_PER_CALL * CHANNELS], U8, tag="scales", align_bytes=64)
             words = grouped[(b, i)][:].rearrange("p n g c h -> p (n g c h)")
             width = PASSES_PER_CALL * CHANNELS * 2
-            nc.vector.quantize_mx(
-                out=codes[:].bitcast(FP8X4),
-                scales=scales[:],
-                in_=words[:, part_call * width : (part_call + 1) * width].bitcast(BF16),
-            )
+            parts = 2 if (b, k) == (IMAGES - 1, CALLS_PER_IMAGE - 1) else 1
+            for h in range(parts):
+                w_cols = width // parts
+                c_cols = PASSES_PER_CALL * CHANNELS // parts
+                nc.vector.quantize_mx(
+                    out=codes[:, h * c_cols : (h + 1) * c_cols].bitcast(FP8X4),
+                    scales=scales[:, h * c_cols : (h + 1) * c_cols],
+                    in_=words[
+                        :, part_call * width + h * w_cols : part_call * width + (h + 1) * w_cols
+                    ].bitcast(BF16),
+                )
             quantised[(b, k)] = (codes, scales)
 
         def multiply(b, k):
@@ -301,9 +307,9 @@ def tile_covpool_k_kernel(tc, x, out):
         for u in range(UNITS):
             end = (u + 1) * PIECES_PER_UNIT - 1
             to_spread.setdefault(end + SPREAD_LAG, []).append(u)
-            to_join.setdefault(end + JOIN_LAG, []).append(u)
-            to_finish.setdefault(end + MEAN_LAG - 1, []).append(u)
-            mean_step[u] = end + MEAN_LAG
+            to_join.setdefault(end + (JOIN_LAG if u < UNITS - 1 else SPREAD_LAG), []).append(u)
+            mean_step[u] = end + MEAN_LAG - (1 if u == UNITS - 1 else 0)
+            to_finish.setdefault(mean_step[u] - 1, []).append(u)
         step = 0
         for p in ORDER:
             step = max(step, mean_step[p // PIECES_PER_UNIT])
@@ -312,6 +318,7 @@ def tile_covpool_k_kernel(tc, x, out):
             to_group[step + GR_LAG] = p
             group_step[p] = step + GR_LAG
             step += 1
+        last_transpose = max(to_transpose)
         call_step = {}
         step = 0
         for b in range(IMAGES):
@@ -328,6 +335,8 @@ def tile_covpool_k_kernel(tc, x, out):
         step = 0
         for s in sorted(call_step):
             step = max(step, s + MULTIPLY_LAG)
+            if step == last_transpose - 1:
+                step = last_transpose
             multiply_at.setdefault(step, []).append(call_step[s])
         last_step = max(multiply_at) + 1
 
@@ -338,13 +347,17 @@ def tile_covpool_k_kernel(tc, x, out):
             for u in to_spread.get(s, []):
                 spread(u)
             for u in to_join.get(s, []):
-                mean_parts_of[u] = join(u)
+                if u < UNITS - 1:
+                    mean_parts_of[u] = join(u)
             if s in to_centre:
                 centre(*divmod(to_centre[s], PIECES_PER_UNIT))
             for u in to_finish.get(s, []):
                 finish_mean(u, mean_parts_of[u])
             if s in to_transpose:
                 transpose(*divmod(to_transpose[s], PIECES_PER_UNIT))
+            for u in to_join.get(s, []):
+                if u == UNITS - 1:
+                    mean_parts_of[u] = join(u)
             if s in to_group:
                 group(*divmod(to_group[s], PIECES_PER_UNIT))
             for call in multiply_at.get(s, []):

@@ -33,8 +33,8 @@ PASSES_PER_PIECE = PARTS * PIECE_COLS // 512
 PASSES_PER_CALL = 8
 CALLS_PER_PIECE = PASSES_PER_PIECE // PASSES_PER_CALL
 CALLS_PER_IMAGE = PIECES_PER_UNIT * CALLS_PER_PIECE
-TENSOR_COLS = (0, 256, 1280, 1280)
-VECTOR_COLS = (1216, 1536, 512, 512)
+TENSOR_COLS = (0, 384, 1280, 1280)
+VECTOR_COLS = (1216, 1408, 512, 512)
 
 
 def tensor_cols(u):
@@ -45,19 +45,11 @@ def vector_cols(u):
     return VECTOR_COLS[u // UNITS_PER_IMAGE]
 
 
-def scalar_cols(u):
-    return PIECE_COLS - tensor_cols(u) - vector_cols(u)
-
-
 WHOLE = (False, True, True, True)
 
 
 def addends_of(u):
-    return adders(u) * (1 if WHOLE[u // UNITS_PER_IMAGE] else PIECES_PER_UNIT)
-
-
-def adders(u):
-    return 2 if scalar_cols(u) else 1
+    return PIECES_PER_UNIT + (1 if WHOLE[u // UNITS_PER_IMAGE] else PIECES_PER_UNIT)
 
 
 SPREAD_LAG = 1
@@ -156,34 +148,29 @@ def tile_covpool_k_kernel(tc, x, out):
 
         def add_up(u, i):
             first = tensor_cols(u)
-            if WHOLE[u // UNITS_PER_IMAGE]:
-                if i < PIECES_PER_UNIT - 1:
-                    return
-                piece = x_sb[u][:].rearrange("p (i n) -> p i n", i=PIECES_PER_UNIT)
-                cols_v = piece[:, :, first : first + vector_cols(u)]
-                cols_s = piece[:, :, first + vector_cols(u) :]
-                i = 0
-            else:
-                piece = piece_of(u, i)
-                cols_v = piece[:, first : first + vector_cols(u)]
-                cols_s = piece[:, first + vector_cols(u) :]
-            a = adders(u)
+            second = first + vector_cols(u)
+            piece = piece_of(u, i)
             nc.vector.tensor_scalar(
-                out=cols_v,
-                in0=cols_v,
+                out=piece[:, first:second],
+                in0=piece[:, first:second],
                 scalar1=1.0,
                 scalar2=None,
                 op0=ALU.mult,
                 op1=ALU.add,
-                accum_out=addends[u][:, a * i : a * i + 1],
+                accum_out=addends[u][:, i : i + 1],
             )
-            if a == 2:
-                nc.scalar.activation(
-                    out=cols_s,
-                    in_=cols_s,
-                    func=ACT.Copy,
-                    accum_out=addends[u][:, a * i + 1 : a * i + 2],
-                )
+            if not WHOLE[u // UNITS_PER_IMAGE]:
+                cols = piece[:, second:]
+                column = PIECES_PER_UNIT + i
+            elif i == PIECES_PER_UNIT - 1:
+                unit = x_sb[u][:].rearrange("p (i n) -> p i n", i=PIECES_PER_UNIT)
+                cols = unit[:, :, second:]
+                column = PIECES_PER_UNIT
+            else:
+                return
+            nc.scalar.activation(
+                out=cols, in_=cols, func=ACT.Copy, accum_out=addends[u][:, column : column + 1]
+            )
 
         def spread(u):
             if tensor_cols(u) == 0:

@@ -33,8 +33,8 @@ PASSES_PER_PIECE = PARTS * PIECE_COLS // 512
 PASSES_PER_CALL = 8
 CALLS_PER_PIECE = PASSES_PER_PIECE // PASSES_PER_CALL
 CALLS_PER_IMAGE = PIECES_PER_UNIT * CALLS_PER_PIECE
-TENSOR_COLS = (0, 384, 1280, 1280)
-VECTOR_COLS = (1216, 1408, 512, 512)
+TENSOR_COLS = (0, 384, 1280, 1408)
+VECTOR_COLS = (1216, 1408, 512, 448)
 
 
 def tensor_cols(u):

from contextlib import ExitStack

import concourse.mybir as mybir
from concourse.masks import make_identity

F32 = mybir.dt.float32
BF16 = mybir.dt.bfloat16
U32 = mybir.dt.uint32
U8 = mybir.dt.uint8
FP8X4 = mybir.dt.float8_e4m3fn_x4
ALU = mybir.AluOpType
ACT = mybir.ActivationFunctionType
AXIS = mybir.AxisListType

IMAGES = 4
CHANNELS = 128
POSITIONS = 16384
FLOPS = 2 * IMAGES * CHANNELS * CHANNELS * POSITIONS

P = 128
PARTS = 4
UNIT_CHANNELS = P // PARTS
UNITS_PER_IMAGE = CHANNELS // UNIT_CHANNELS
UNITS = IMAGES * UNITS_PER_IMAGE
UNIT_COLS = POSITIONS // PARTS
PIECE_COLS = 2048
PIECES_PER_UNIT = UNIT_COLS // PIECE_COLS
PIECES_PER_IMAGE = UNITS_PER_IMAGE * PIECES_PER_UNIT
PIECES = UNITS * PIECES_PER_UNIT
STRETCHES_PER_BANK = 2
BANKS_PER_PIECE = PIECE_COLS // (512 * STRETCHES_PER_BANK)
PASSES_PER_PIECE = PARTS * PIECE_COLS // 512
PASSES_PER_CALL = 8
CALLS_PER_PIECE = PASSES_PER_PIECE // PASSES_PER_CALL
CALLS_PER_IMAGE = PIECES_PER_UNIT * CALLS_PER_PIECE
TENSOR_COLS = (0, 384, 1280, 1408)
VECTOR_COLS = (1216, 1408, 512, 448)


def tensor_cols(u):
    return TENSOR_COLS[u // UNITS_PER_IMAGE]


def vector_cols(u):
    return VECTOR_COLS[u // UNITS_PER_IMAGE]


WHOLE = (False, True, True, True)


def addends_of(u):
    return PIECES_PER_UNIT + (1 if WHOLE[u // UNITS_PER_IMAGE] else PIECES_PER_UNIT)


SPREAD_LAG = 1
JOIN_LAG = 2
CALL_GAP = 2
CALL_LAG = 2
MULTIPLY_LAG = 1
MEAN_LAG = 4
ORDER = list(range(PIECES - 4)) + [PIECES - 4, PIECES - 2, PIECES - 3, PIECES - 1]
TR_LAG = 1
GR_LAG = 2


def tile_covpool_k_kernel(tc, x, out):
    nc = tc.nc
    x_rows = x.rearrange("b c (j h) w -> (b c j) (h w)", j=PARTS)

    with ExitStack() as ctx:
        consts = ctx.enter_context(tc.tile_pool(name="consts", bufs=1))
        resident = ctx.enter_context(tc.tile_pool(name="resident", bufs=1))
        grouped_pool = ctx.enter_context(tc.tile_pool(name="grouped", bufs=2 * PIECES_PER_UNIT))
        mx_pool = ctx.enter_context(tc.tile_pool(name="mx", bufs=6))
        small = ctx.enter_context(tc.tile_pool(name="small", bufs=4))
        work_psum = ctx.enter_context(tc.psum_pool(name="work_psum", bufs=4))
        sums_psum = ctx.enter_context(tc.psum_pool(name="sums_psum", bufs=1))
        mean_psum = ctx.enter_context(tc.psum_pool(name="mean_psum", bufs=1))
        acc_psum = ctx.enter_context(tc.psum_pool(name="acc_psum", bufs=2))
        ctx.enter_context(tc.manual_schedule())

        x_sb = []
        for u in range(UNITS):
            x_unit = resident.tile([P, UNIT_COLS], BF16, name="x_unit%d" % u)
            x_sb.append(x_unit)
            for i in range(PIECES_PER_UNIT):
                cols = slice(i * PIECE_COLS, (i + 1) * PIECE_COLS)
                nc.sync.dma_start(out=x_unit[:, cols], in_=x_rows[u * P : (u + 1) * P, cols])

        one_over_positions = consts.tile([P, 1], F32)
        nc.vector.memset(one_over_positions[:], 1.0 / POSITIONS)
        first_copy = consts.tile([P, 1], F32)
        nc.scalar.activation(out=first_copy[:], in_=one_over_positions[:], func=ACT.Copy)
        ident = consts.tile([P, P], F32)
        make_identity(nc, ident[:])
        own_channel = consts.tile([P, UNIT_CHANNELS], F32)
        nc.vector.tensor_reduce(
            out=own_channel[:],
            in_=ident[:].rearrange("q (c j) -> q c j", j=PARTS),
            axis=AXIS.X,
            op=ALU.add,
        )
        own_channel_bf = consts.tile([P, UNIT_CHANNELS], BF16)
        nc.vector.tensor_copy(out=own_channel_bf[:], in_=own_channel[:])
        part_averaging = consts.tile([P, UNIT_CHANNELS, PARTS], F32)
        nc.vector.tensor_scalar(
            out=part_averaging[:],
            in0=own_channel[:].unsqueeze(2).to_broadcast([P, UNIT_CHANNELS, PARTS]),
            scalar1=1.0 / POSITIONS,
            scalar2=None,
            op0=ALU.mult,
        )
        ident_by_part = consts.tile([P, PARTS, UNIT_CHANNELS], F32)
        nc.vector.tensor_copy(
            out=ident_by_part[:], in_=ident[:].rearrange("q (c j) -> q j c", j=PARTS)
        )

        addends = [
            resident.tile([P, addends_of(u)], F32, name="addends%d" % u) for u in range(UNITS)
        ]
        means = [resident.tile([P, 1], F32, name="mean%d" % u) for u in range(UNITS)]
        column_sums = {}
        spread_sums = {}
        banks = {}
        grouped = {}
        quantised = {}
        acc = {}

        def piece_of(u, i):
            return x_sb[u][:, i * PIECE_COLS : (i + 1) * PIECE_COLS]

        def tensor_add_up(u, i):
            if tensor_cols(u) == 0:
                return
            if i == 0:
                sums = sums_psum.tile([P, UNIT_CHANNELS], F32, tag="column_sums")
                column_sums[u] = sums
            piece = piece_of(u, i)
            blocks = tensor_cols(u) // P
            for k in range(blocks):
                nc.tensor.matmul(
                    out=column_sums[u][:],
                    lhsT=piece[:, k * P : (k + 1) * P],
                    rhs=own_channel_bf[:],
                    start=(i == 0 and k == 0),
                    stop=(i == PIECES_PER_UNIT - 1 and k == blocks - 1),
                )

        def add_up(u, i):
            first = tensor_cols(u)
            second = first + vector_cols(u)
            piece = piece_of(u, i)
            nc.vector.tensor_scalar(
                out=piece[:, first:second],
                in0=piece[:, first:second],
                scalar1=1.0,
                scalar2=None,
                op0=ALU.mult,
                op1=ALU.add,
                accum_out=addends[u][:, i : i + 1],
            )
            if not WHOLE[u // UNITS_PER_IMAGE]:
                cols = piece[:, second:]
                column = PIECES_PER_UNIT + i
            elif i == PIECES_PER_UNIT - 1:
                unit = x_sb[u][:].rearrange("p (i n) -> p i n", i=PIECES_PER_UNIT)
                cols = unit[:, :, second:]
                column = PIECES_PER_UNIT
            else:
                return
            nc.scalar.activation(
                out=cols, in_=cols, func=ACT.Copy, accum_out=addends[u][:, column : column + 1]
            )

        def spread(u):
            if tensor_cols(u) == 0:
                return
            repeated = small.tile([P, UNIT_CHANNELS, PARTS], F32, tag="spread")
            spread_sums[u] = repeated
            nc.scalar.copy(
                out=repeated[:],
                in_=column_sums[u][:].unsqueeze(2).to_broadcast([P, UNIT_CHANNELS, PARTS]),
            )

        def join(u):
            parts = addends_of(u)
            if tensor_cols(u):
                parts += 1
            mean_parts = mean_psum.tile([P, parts], F32, tag="mean_parts")
            nc.tensor.matmul(
                out=mean_parts[:, : addends_of(u)],
                lhsT=part_averaging[:].rearrange("p c j -> p (c j)"),
                rhs=addends[u][:],
                start=True,
                stop=True,
            )
            if tensor_cols(u):
                nc.tensor.matmul(
                    out=mean_parts[:, parts - 1 :],
                    lhsT=spread_sums[u][:].rearrange("p c j -> p (c j)"),
                    rhs=one_over_positions[:],
                    start=True,
                    stop=True,
                )
            return mean_parts

        def finish_mean(u, mean_parts):
            nc.vector.tensor_reduce(out=means[u][:], in_=mean_parts[:], axis=AXIS.X, op=ALU.add)

        def centre(u, i):
            piece = piece_of(u, i)
            nc.vector.tensor_scalar(
                out=piece, in0=piece, scalar1=means[u][:, 0:1], scalar2=None, op0=ALU.subtract
            )

        def transpose(u, i):
            words = x_sb[u][:].bitcast(F32)
            banks[(u, i)] = []
            for n in range(BANKS_PER_PIECE):
                bank = work_psum.tile(
                    [P, PARTS, STRETCHES_PER_BANK, 2, UNIT_CHANNELS], F32, tag="work"
                )
                for s in range(STRETCHES_PER_BANK):
                    for h in range(2):
                        stretch = (i * BANKS_PER_PIECE + n) * STRETCHES_PER_BANK + s
                        first = (2 * stretch + h) * P
                        nc.tensor.transpose(
                            bank[:, :, s, h, :],
                            words[:, first : first + P],
                            ident_by_part[:].rearrange("q j c -> q (j c)"),
                        )
                banks[(u, i)].append(bank)

        def group(u, i):
            b, r = divmod(u, UNITS_PER_IMAGE)
            if (b, i) not in grouped:
                grouped_tile = grouped_pool.tile(
                    [P, BANKS_PER_PIECE, PARTS * STRETCHES_PER_BANK, CHANNELS, 2],
                    F32,
                    tag="grouped",
                    align_bytes=64,
                )
                grouped[(b, i)] = grouped_tile
            for n in range(BANKS_PER_PIECE):
                nc.scalar.copy(
                    out=grouped[(b, i)][:, n, :, r * UNIT_CHANNELS : (r + 1) * UNIT_CHANNELS, :],
                    in_=banks[(u, i)][n][:].rearrange("p j s h c -> p (j s) c h"),
                )

        def quantise(b, k):
            i, part_call = divmod(k, CALLS_PER_PIECE)
            codes = mx_pool.tile([P, PASSES_PER_CALL * CHANNELS], U32, tag="codes", align_bytes=64)
            scales = mx_pool.tile([P, PASSES_PER_CALL * CHANNELS], U8, tag="scales", align_bytes=64)
            words = grouped[(b, i)][:].rearrange("p n g c h -> p (n g c h)")
            width = PASSES_PER_CALL * CHANNELS * 2
            parts = 2 if (b, k) == (IMAGES - 1, CALLS_PER_IMAGE - 1) else 1
            for h in range(parts):
                w_cols = width // parts
                c_cols = PASSES_PER_CALL * CHANNELS // parts
                nc.vector.quantize_mx(
                    out=codes[:, h * c_cols : (h + 1) * c_cols].bitcast(FP8X4),
                    scales=scales[:, h * c_cols : (h + 1) * c_cols],
                    in_=words[
                        :, part_call * width + h * w_cols : part_call * width + (h + 1) * w_cols
                    ].bitcast(BF16),
                )
            quantised[(b, k)] = (codes, scales)

        def multiply(b, k):
            if k == 0:
                acc_tile = acc_psum.tile([CHANNELS, CHANNELS], F32, tag="acc")
                acc[b] = acc_tile
            codes, scales = quantised[(b, k)]
            for g in range(PASSES_PER_CALL):
                cols = slice(g * CHANNELS, (g + 1) * CHANNELS)
                nc.tensor.matmul_mx(
                    out=acc[b][:],
                    lhsT=codes[:, cols].bitcast(FP8X4),
                    lhsT_scale=scales[:, cols],
                    rhs=codes[:, cols].bitcast(FP8X4),
                    rhs_scale=scales[:, cols],
                    start=(k == 0 and g == 0),
                    stop=(k == CALLS_PER_IMAGE - 1 and g == PASSES_PER_CALL - 1),
                )

        def store(b):
            y_sb = small.tile([CHANNELS, CHANNELS], F32, tag="y")
            nc.scalar.activation(out=y_sb[:], in_=acc[b][:], func=ACT.Copy, scale=1.0 / POSITIONS)
            nc.sync.dma_start(out=out[b], in_=y_sb[:])

        to_spread, to_join, to_finish = {}, {}, {}
        to_centre, to_transpose, to_group, group_step = {}, {}, {}, {}
        mean_step = {}
        for u in range(UNITS):
            end = (u + 1) * PIECES_PER_UNIT - 1
            to_spread.setdefault(end + SPREAD_LAG, []).append(u)
            to_join.setdefault(end + (JOIN_LAG if u < UNITS - 1 else SPREAD_LAG), []).append(u)
            mean_step[u] = end + MEAN_LAG - (1 if u == UNITS - 1 else 0)
            to_finish.setdefault(mean_step[u] - 1, []).append(u)
        step = 0
        for p in ORDER:
            step = max(step, mean_step[p // PIECES_PER_UNIT])
            to_centre[step] = p
            to_transpose[step + TR_LAG] = p
            to_group[step + GR_LAG] = p
            group_step[p] = step + GR_LAG
            step += 1
        last_transpose = max(to_transpose)
        call_step = {}
        step = 0
        for b in range(IMAGES):
            for k in range(CALLS_PER_IMAGE):
                i = k // CALLS_PER_PIECE
                ready = max(
                    group_step[b * PIECES_PER_IMAGE + r * PIECES_PER_UNIT + i]
                    for r in range(UNITS_PER_IMAGE)
                )
                step = max(step, ready + CALL_LAG)
                call_step[step] = (b, k)
                step += CALL_GAP if step < PIECES else 1
        multiply_at = {}
        step = 0
        for s in sorted(call_step):
            step = max(step, s + MULTIPLY_LAG)
            if step == last_transpose - 1:
                step = last_transpose
            multiply_at.setdefault(step, []).append(call_step[s])
        last_step = max(multiply_at) + 1

        mean_parts_of = {}
        for s in range(last_step + 1):
            if s in call_step:
                quantise(call_step[s][0], call_step[s][1])
            for u in to_spread.get(s, []):
                spread(u)
            for u in to_join.get(s, []):
                if u < UNITS - 1:
                    mean_parts_of[u] = join(u)
            if s in to_centre:
                centre(*divmod(to_centre[s], PIECES_PER_UNIT))
            for u in to_finish.get(s, []):
                finish_mean(u, mean_parts_of[u])
            if s in to_transpose:
                transpose(*divmod(to_transpose[s], PIECES_PER_UNIT))
            for u in to_join.get(s, []):
                if u == UNITS - 1:
                    mean_parts_of[u] = join(u)
            if s in to_group:
                group(*divmod(to_group[s], PIECES_PER_UNIT))
            for call in multiply_at.get(s, []):
                multiply(call[0], call[1])
            for call in multiply_at.get(s - 1, []):
                if call[1] == CALLS_PER_IMAGE - 1:
                    store(call[0])
            if s < PIECES:
                tensor_add_up(*divmod(s, PIECES_PER_UNIT))
                add_up(*divmod(s, PIECES_PER_UNIT))
